import numpy as np
import ml_dtypes


def mxq(x, axis, fmt="e4m3"):
    dtype, down = {"e4m3": (ml_dtypes.float8_e4m3fn, 7), "e5m2": (ml_dtypes.float8_e5m2, 14)}[fmt]
    v = np.moveaxis(np.asarray(x, np.float32).astype(ml_dtypes.bfloat16).astype(np.float64), axis, -1)
    blocks = v.reshape(v.shape[:-1] + (-1, 32))
    amax = np.abs(blocks).max(-1, keepdims=True)
    byte = np.maximum(np.where(amax > 0, np.frexp(amax)[1] - 1 + 127, 0) - down, 1)
    scale = np.exp2(byte - 127.0)
    codes = (blocks / scale).astype(np.float32).astype(dtype).astype(np.float64)
    return np.moveaxis((codes * scale).reshape(v.shape), -1, axis)


WIDE = False


def mx_kscale(k):
    if not WIDE:
        return np.ones(k)
    levels = np.array([10, -10, 5, -5, 0])
    a = np.random.permutation(np.resize(levels, k // 512 * 4)).reshape(k // 512, 4)
    idx = np.arange(k)
    return np.exp2(a[idx // 512, idx % 128 // 32])


BF16 = ml_dtypes.bfloat16


def bf(x):
    return np.asarray(x, np.float32).astype(BF16)


def f64(x):
    return np.asarray(x).astype(np.float64)


E2M1 = np.array([0.0, 0.5, 1.0, 1.5, 2.0, 3.0, 4.0, 6.0, -0.0, -0.5, -1.0, -1.5, -2.0, -3.0, -4.0, -6.0])


def pack_weight(w, fmt):
    k, n = w.shape
    w = f64(bf(w)).reshape(k // 32, 32, n)
    amax = np.abs(w).max(1)
    if fmt == "e4m3":
        byte = np.frexp(amax)[1] - 1 + 127 - 7
    else:
        mant, ex = np.frexp(amax / 6.0)
        byte = np.where(mant > 0.5, ex, ex - 1) + 127
    byte = np.clip(np.where(amax > 0, byte, 1), 1, 254)
    scaled = (w * np.exp2(127.0 - byte)[:, None, :]).reshape(k, n).astype(np.float32)
    by_word = np.ascontiguousarray(scaled.reshape(k // 512, 128, 4, n).transpose(0, 1, 3, 2))
    if fmt == "e4m3":
        words = by_word.astype(ml_dtypes.float8_e4m3fn).view(np.uint8)
    else:
        c = by_word.astype(ml_dtypes.float4_e2m1fn).view(np.uint8) & 0xF
        words = c[..., 0::2] | (c[..., 1::2] << 4)
    return np.ascontiguousarray(words), np.ascontiguousarray(byte.astype(np.uint8).reshape(k // 512, 16, n))


def unpack_weight(words, scales, fmt):
    g, p, n, _ = words.shape
    if fmt == "e4m3":
        vals = np.ascontiguousarray(words).view(ml_dtypes.float8_e4m3fn).astype(np.float64)
    else:
        nib = np.empty((g, p, n, 4), np.uint8)
        nib[..., 0::2] = words & 0xF
        nib[..., 1::2] = words >> 4
        vals = E2M1[nib]
    vals = vals * np.repeat(np.exp2(scales.astype(np.float64) - 127.0), 8, axis=1)[..., None]
    return vals.transpose(0, 1, 3, 2).reshape(g * 512, n)


B, J, C, K, H, M = 16, 256, 512, 2, 8, 256
DH = C // H
S_G2A, S_A2G = 0.5, 0.8
FMT = "e4m3"


def setup_inputs():
    s = mx_kscale(C)
    attn_o = bf(np.random.standard_normal((B, H, J, DH)) * 0.6 * s.reshape(H, 1, DH))
    xg1 = bf(np.random.standard_normal((B, J, C)) * 0.7 * s)
    x = bf(np.random.standard_normal((B, J, C)))
    adj = bf(np.random.uniform(size=(K, J, J)) / np.sqrt(K * J))
    proj_w_words, proj_w_scales = pack_weight((np.random.standard_normal((C, C)) / np.sqrt(C) / s).T, FMT)
    proj_b = bf(0.1 * np.random.standard_normal(C))
    gcn2_w_words, gcn2_w_scales = pack_weight((np.random.standard_normal((K * C, C)) * 1.5 / np.sqrt(C) / s).T, FMT)
    gcn2_b = bf(np.random.standard_normal(K * C) * 0.6 / np.sqrt(J))
    return {'attn_o': attn_o,
            'xg1': xg1,
            'x': x,
            'adj': adj,
            'proj_w_words': proj_w_words,
            'proj_w_scales': proj_w_scales,
            'proj_b': proj_b,
            'gcn2_w_words': gcn2_w_words,
            'gcn2_w_scales': gcn2_w_scales,
            'gcn2_b': gcn2_b}


def reference(attn_o, xg1, x, adj, proj_w_words, proj_w_scales, proj_b, gcn2_w_words, gcn2_w_scales, gcn2_b):
    o = f64(attn_o)
    g1 = f64(xg1)
    attn2gcn = o.transpose(0, 2, 1, 3).reshape(B, J, C)
    fh = (g1 * S_G2A).reshape(B, J, H, DH).transpose(0, 2, 1, 3)
    v = (o + fh).transpose(0, 2, 1, 3).reshape(B, J, C)
    xa = (mxq(v, 2, 'e4m3') @ unpack_weight(proj_w_words, proj_w_scales, FMT)) + f64(proj_b)
    u = g1 + attn2gcn * S_A2G
    y = (mxq(u, 2, 'e4m3') @ unpack_weight(gcn2_w_words, gcn2_w_scales, FMT)) + f64(gcn2_b)
    yk = y.reshape(B, J, K, C).transpose(0, 2, 1, 3).reshape(B, K * J, C)
    a = f64(adj).reshape(K * J, J)
    xg2 = mxq(a, 0, 'e4m3').T @ mxq(yk, 1, 'e4m3')
    return f64(x) + xg2 + xa

@@ -1,0 +1,250 @@
+from contextlib import ExitStack
+
+import concourse.mybir as mybir
+from concourse.masks import make_identity
+
+F32 = mybir.dt.float32
+BF16 = mybir.dt.bfloat16
+I32 = mybir.dt.int32
+U32 = mybir.dt.uint32
+U8 = mybir.dt.uint8
+FP8X4 = mybir.dt.float8_e4m3fn_x4
+ADD = mybir.AluOpType.add
+COPY = mybir.ActivationFunctionType.Copy
+
+P = 128
+B, J, C, K, H = 16, 256, 512, 2, 8
+DH = C // H
+S_G2A, S_A2G = 0.5, 0.8
+PAR = J // P
+QUARTER = C // 4
+AHEAD = 3
+
+FLOPS = 2 * B * J * C * C + 2 * B * J * C * K * C + 2 * B * J * K * J * C
+
+
+def tile_block_pb_t_kernel(
+    tc, attn_o, xg1, x, adj, proj_w_words, proj_w_scales, proj_b, gcn2_w_words, gcn2_w_scales, gcn2_b, out
+):
+    nc = tc.nc
+    with ExitStack() as ctx:
+        const = ctx.enter_context(tc.tile_pool(name="const", bufs=1))
+        inputs = ctx.enter_context(tc.tile_pool(name="inputs", bufs=AHEAD + 1))
+        work = ctx.enter_context(tc.tile_pool(name="work", bufs=2))
+        results = ctx.enter_context(tc.tile_pool(name="results", bufs=3))
+        psum = ctx.enter_context(tc.psum_pool(name="psum", bufs=1))
+        ctx.enter_context(tc.manual_schedule())
+
+        a_in, g_in, x_in = {}, {}, {}
+
+        def load(b):
+            a_in[b] = inputs.tile([P, PAR, C], BF16, name="a_in")
+            by_parity = attn_o[b].rearrange("h (p e) d -> e p h d", e=PAR)
+            for e in range(PAR):
+                nc.sync.dma_start(out=a_in[b][:, e, :].rearrange("p (h d) -> p h d", h=H), in_=by_parity[e])
+            g_in[b] = inputs.tile([P, PAR, C], BF16, name="g_in")
+            nc.sync.dma_start(
+                out=g_in[b][:].rearrange("p e c -> p (e c)"), in_=xg1[b].rearrange("(p e) c -> p (e c)", e=PAR)
+            )
+            x_in[b] = inputs.tile([P, PAR, C], BF16, name="x_in")
+            nc.sync.dma_start(
+                out=x_in[b][:].rearrange("p e c -> p (e c)"), in_=x[b].rearrange("(p e) c -> p (e c)", e=PAR)
+            )
+
+        w_scales = const.tile([P, C + K * C], U8, align_bytes=64)
+        nc.vector.memset(w_scales[:].bitcast(I32), 0)
+        load(0)
+        for r in range(4):
+            nc.sync.dma_start(out=w_scales[r:P:32, C:].bitcast(I32), in_=gcn2_w_scales[0, r:16:4, :].bitcast(I32))
+        for r in range(4):
+            nc.sync.dma_start(out=w_scales[r:P:32, :C].bitcast(I32), in_=proj_w_scales[0, r:16:4, :].bitcast(I32))
+        gcn2_words = const.tile([P, K * C], U32, align_bytes=64)
+        nc.sync.dma_start(
+            out=gcn2_words[:].bitcast(I32), in_=gcn2_w_words[0].rearrange("p n t -> p (n t)").bitcast(I32)
+        )
+        proj_words = const.tile([P, C], U32, align_bytes=64)
+        nc.sync.dma_start(
+            out=proj_words[:].bitcast(I32), in_=proj_w_words[0].rearrange("p n t -> p (n t)").bitcast(I32)
+        )
+        adj_raw = const.tile([P, K * PAR, J], BF16)
+        nc.sync.dma_start(
+            out=adj_raw[:].rearrange("p (k e) w -> p k (e w)", k=K), in_=adj.rearrange("k (p e) w -> p k (e w)", e=PAR)
+        )
+        for b in range(1, AHEAD):
+            load(b)
+
+        gcn2_b_rows = const.tile([P, K * C], BF16)
+        nc.scalar.dma_start(out=gcn2_b_rows[:], in_=gcn2_b.partition_broadcast(P))
+        proj_b_rows = const.tile([P, C], BF16)
+        nc.scalar.dma_start(out=proj_b_rows[:], in_=proj_b.partition_broadcast(P))
+
+        identity = const.tile([P, P], F32)
+        make_identity(nc, identity[:])
+
+        y_bias = const.tile([P, C * K * PAR], BF16)
+        nc.vector.tensor_copy(
+            out=y_bias[:].rearrange("p (c k e) -> p c k e", k=K, e=PAR),
+            in_=gcn2_b_rows[:].rearrange("p (k c) -> p c k", k=K).unsqueeze(3).to_broadcast([P, C, K, PAR]),
+        )
+
+        adj_codes = const.tile([P, J], U32, align_bytes=64)
+        adj_scales = const.tile([P, J], U8, align_bytes=64)
+
+        def quantise_adj():
+            adj_grouped = const.tile([P, J * K * PAR], BF16, align_bytes=64)
+            nc.vector.tensor_copy(
+                out=adj_grouped[:].rearrange("p (f m t) -> p f m t", f=PAR, t=K * PAR),
+                in_=adj_raw[:].rearrange("p t (m f) -> p f m t", f=PAR),
+            )
+            nc.vector.quantize_mx(out=adj_codes[:].bitcast(FP8X4), scales=adj_scales[:], in_=adj_grouped[:])
+
+        a_t, g_t, a_scaled, g_scaled, vu, vu_codes, vu_scales = {}, {}, {}, {}, {}, {}, {}
+        y_banks, y_codes, y_scales, x_biased = {}, {}, {}, {}
+
+        def pairs_by_token(bank):
+            halves = bank[:].rearrange("m s n -> m (s n)").bitcast(BF16)
+            return halves.rearrange("m (s n i) -> m n s i", s=2, i=2)
+
+        def by_token(ap):
+            return ap.rearrange("m (n s i) -> m n s i", s=2, i=2)
+
+        def transpose(b):
+            for name, source, banks in (("a_t", a_in, a_t), ("g_t", g_in, g_t)):
+                banks[b] = psum.tile([P, 2, J], F32, name=name)
+                words = source[b][:].rearrange("p e c -> p (e c)").bitcast(F32)
+                for e in range(PAR):
+                    for s in range(2):
+                        first = e * (C // 2) + s
+                        nc.tensor.transpose(
+                            banks[b][:, s, e * P : (e + 1) * P], words[:, first : (e + 1) * (C // 2) : 2], identity[:]
+                        )
+
+        def scale(b):
+            a_scaled[b] = work.tile([P, 4 * J], F32, name="a_scaled")
+            nc.scalar.activation(out=by_token(a_scaled[b][:]), in_=pairs_by_token(a_t[b]), func=COPY, scale=S_A2G)
+            g_scaled[b] = work.tile([P, 4 * J], BF16, name="g_scaled")
+            nc.scalar.activation(out=by_token(g_scaled[b][:]), in_=pairs_by_token(g_t[b]), func=COPY, scale=S_G2A)
+
+        def combine_v(b):
+            vu[b] = work.tile([P, 2, 4 * J], BF16, name="vu", align_bytes=64)
+            nc.vector.tensor_tensor(
+                out=by_token(vu[b][:, 0, :]), in0=pairs_by_token(a_t[b]), in1=by_token(g_scaled[b][:]), op=ADD
+            )
+
+        def combine_u(b):
+            nc.vector.tensor_tensor(
+                out=by_token(vu[b][:, 1, :]), in0=pairs_by_token(g_t[b]), in1=by_token(a_scaled[b][:]), op=ADD
+            )
+
+        def quantise_vu(b):
+            vu_codes[b] = work.tile([P, 2 * J], U32, name="vu_codes", align_bytes=64)
+            vu_scales[b] = work.tile([P, 2 * J], U8, name="vu_scales", align_bytes=64)
+            nc.vector.quantize_mx(
+                out=vu_codes[b][:].bitcast(FP8X4), scales=vu_scales[b][:], in_=vu[b][:].rearrange("m o n -> m (o n)")
+            )
+
+        def bias_x(b):
+            x_biased[b] = results.tile([P, PAR, C], F32, name="x_biased")
+            nc.gpsimd.tensor_tensor(
+                out=x_biased[b][:], in0=x_in[b][:], in1=proj_b_rows[:].unsqueeze(1).to_broadcast([P, PAR, C]), op=ADD
+            )
+
+        def multiply_y(b):
+            y_banks[b] = []
+            for q in range(4):
+                bank = psum.tile([P, K * PAR, QUARTER], F32, name="y_bank%d" % q)
+                y_banks[b].append(bank)
+                for e in range(PAR):
+                    tokens = slice(J + e * P, J + (e + 1) * P)
+                    for k in range(K):
+                        first = k * C + q * QUARTER
+                        nc.tensor.matmul_mx(
+                            out=bank[:, k * PAR + e, :],
+                            lhsT=vu_codes[b][:, tokens].bitcast(FP8X4),
+                            lhsT_scale=vu_scales[b][:, tokens],
+                            rhs=gcn2_words[:, first : first + QUARTER].bitcast(FP8X4),
+                            rhs_scale=w_scales[:, C + first : C + first + QUARTER],
+                            start=True,
+                            stop=True,
+                        )
+
+        y_grouped = {}
+
+        def bias_y(b):
+            y_grouped[b] = work.tile([P, 4 * C], BF16, name="y_grouped", align_bytes=64)
+            for q in range(4):
+                part = slice(q * 4 * QUARTER, (q + 1) * 4 * QUARTER)
+                nc.vector.tensor_tensor(
+                    out=y_grouped[b][:, part].rearrange("p (c t) -> p c t", t=4),
+                    in0=y_banks[b][q][:].rearrange("p t c -> p c t"),
+                    in1=y_bias[:, part].rearrange("p (c t) -> p c t", t=4),
+                    op=ADD,
+                )
+
+        def quantise_y(b):
+            y_codes[b] = work.tile([P, C], U32, name="y_codes", align_bytes=64)
+            y_scales[b] = work.tile([P, C], U8, name="y_scales", align_bytes=64)
+            nc.vector.quantize_mx(out=y_codes[b][:].bitcast(FP8X4), scales=y_scales[b][:], in_=y_grouped[b][:])
+
+        out_banks = {}
+
+        def multiply_out(b):
+            out_banks[b] = []
+            for f in range(PAR):
+                bank = psum.tile([P, C], F32, name="out_bank%d" % f)
+                out_banks[b].append(bank)
+                tokens = slice(f * P, (f + 1) * P)
+                nc.tensor.matmul_mx(
+                    out=bank[:],
+                    lhsT=vu_codes[b][:, tokens].bitcast(FP8X4),
+                    lhsT_scale=vu_scales[b][:, tokens],
+                    rhs=proj_words[:].bitcast(FP8X4),
+                    rhs_scale=w_scales[:, :C],
+                    start=True,
+                    stop=False,
+                )
+                nc.tensor.matmul_mx(
+                    out=bank[:],
+                    lhsT=adj_codes[:, tokens].bitcast(FP8X4),
+                    lhsT_scale=adj_scales[:, tokens],
+                    rhs=y_codes[b][:].bitcast(FP8X4),
+                    rhs_scale=y_scales[b][:],
+                    start=False,
+                    stop=True,
+                )
+
+        def finish(b):
+            result = results.tile([P, PAR, C], F32, name="result")
+            for f in range(PAR):
+                nc.vector.tensor_tensor(out=result[:, f, :], in0=out_banks[b][f][:], in1=x_biased[b][:, f, :], op=ADD)
+            nc.sync.dma_start(
+                out=out[b].rearrange("(p e) c -> p (e c)", e=PAR), in_=result[:].rearrange("p e c -> p (e c)")
+            )
+
+        transpose(0)
+        scale(0)
+        combine_v(0)
+        combine_u(0)
+        quantise_vu(0)
+        quantise_adj()
+        bias_x(0)
+        bias_x(1)
+        for b in range(B):
+            following = b + 1 < B
+            if b + AHEAD < B:
+                load(b + AHEAD)
+            if b + 2 < B:
+                bias_x(b + 2)
+            if following:
+                transpose(b + 1)
+                scale(b + 1)
+            multiply_y(b)
+            bias_y(b)
+            if following:
+                combine_v(b + 1)
+            quantise_y(b)
+            multiply_out(b)
+            if following:
+                combine_u(b + 1)
+                quantise_vu(b + 1)
+            finish(b)

@@ -18,7 +18,7 @@ DH = C // H
 S_G2A, S_A2G = 0.5, 0.8
 PAR = J // P
 QUARTER = C // 4
-AHEAD = 3
+AHEAD = 4
 
 FLOPS = 2 * B * J * C * C + 2 * B * J * C * K * C + 2 * B * J * K * J * C
 
@@ -29,7 +29,7 @@ def tile_block_pb_t_kernel(
     nc = tc.nc
     with ExitStack() as ctx:
         const = ctx.enter_context(tc.tile_pool(name="const", bufs=1))
-        inputs = ctx.enter_context(tc.tile_pool(name="inputs", bufs=AHEAD + 1))
+        inputs = ctx.enter_context(tc.tile_pool(name="inputs", bufs=AHEAD))
         work = ctx.enter_context(tc.tile_pool(name="work", bufs=2))
         results = ctx.enter_context(tc.tile_pool(name="results", bufs=3))
         psum = ctx.enter_context(tc.psum_pool(name="psum", bufs=1))
@@ -98,7 +98,7 @@ def tile_block_pb_t_kernel(
             )
             nc.vector.quantize_mx(out=adj_codes[:].bitcast(FP8X4), scales=adj_scales[:], in_=adj_grouped[:])
 
-        a_t, g_t, a_scaled, g_scaled, vu, vu_codes, vu_scales = {}, {}, {}, {}, {}, {}, {}
+        a_t, g_t, a_scaled, g_scaled, g_plain, vu, vu_codes, vu_scales = {}, {}, {}, {}, {}, {}, {}, {}
         y_banks, y_codes, y_scales, x_biased = {}, {}, {}, {}
 
         def pairs_by_token(bank):
@@ -122,19 +122,21 @@ def tile_block_pb_t_kernel(
         def scale(b):
             a_scaled[b] = work.tile([P, 4 * J], F32, name="a_scaled")
             nc.scalar.activation(out=by_token(a_scaled[b][:]), in_=pairs_by_token(a_t[b]), func=COPY, scale=S_A2G)
+            g_plain[b] = work.tile([P, 4 * J], BF16, name="g_plain")
+            nc.scalar.copy(
+                out=g_plain[b][:].bitcast(F32).rearrange("m (n s) -> m n s", s=2), in_=g_t[b][:].rearrange("m s n -> m n s")
+            )
             g_scaled[b] = work.tile([P, 4 * J], BF16, name="g_scaled")
             nc.scalar.activation(out=by_token(g_scaled[b][:]), in_=pairs_by_token(g_t[b]), func=COPY, scale=S_G2A)
 
         def combine_v(b):
-            vu[b] = work.tile([P, 2, 4 * J], BF16, name="vu", align_bytes=64)
             nc.vector.tensor_tensor(
                 out=by_token(vu[b][:, 0, :]), in0=pairs_by_token(a_t[b]), in1=by_token(g_scaled[b][:]), op=ADD
             )
 
         def combine_u(b):
-            nc.vector.tensor_tensor(
-                out=by_token(vu[b][:, 1, :]), in0=pairs_by_token(g_t[b]), in1=by_token(a_scaled[b][:]), op=ADD
-            )
+            vu[b] = work.tile([P, 2, 4 * J], BF16, name="vu", align_bytes=64)
+            nc.gpsimd.tensor_tensor(out=vu[b][:, 1, :], in0=g_plain[b][:], in1=a_scaled[b][:], op=ADD)
 
         def quantise_vu(b):
             vu_codes[b] = work.tile([P, 2 * J], U32, name="vu_codes", align_bytes=64)
@@ -221,30 +223,33 @@ def tile_block_pb_t_kernel(
                 out=out[b].rearrange("(p e) c -> p (e c)", e=PAR), in_=result[:].rearrange("p e c -> p (e c)")
             )
 
-        transpose(0)
-        scale(0)
+        def prepare(b):
+            transpose(b)
+            scale(b)
+            combine_u(b)
+
+        prepare(0)
         combine_v(0)
-        combine_u(0)
+        prepare(1)
         quantise_vu(0)
+        combine_v(1)
+        multiply_y(0)
         quantise_adj()
         bias_x(0)
         bias_x(1)
         for b in range(B):
-            following = b + 1 < B
             if b + AHEAD < B:
                 load(b + AHEAD)
             if b + 2 < B:
+                prepare(b + 2)
                 bias_x(b + 2)
-            if following:
-                transpose(b + 1)
-                scale(b + 1)
-            multiply_y(b)
             bias_y(b)
-            if following:
-                combine_v(b + 1)
-            quantise_y(b)
-            multiply_out(b)
-            if following:
-                combine_u(b + 1)
+            if b + 1 < B:
                 quantise_vu(b + 1)
+            quantise_y(b)
+            if b + 2 < B:
+                combine_v(b + 2)
+            multiply_out(b)
+            if b + 1 < B:
+                multiply_y(b + 1)
             finish(b)

@@ -139,8 +139,8 @@ def tile_block_pb_t_kernel(
             nc.gpsimd.tensor_tensor(out=vu[b][:, 1, :], in0=g_plain[b][:], in1=a_scaled[b][:], op=ADD)
 
         def quantise_vu(b):
-            vu_codes[b] = work.tile([P, 2 * J], U32, name="vu_codes", align_bytes=64)
-            vu_scales[b] = work.tile([P, 2 * J], U8, name="vu_scales", align_bytes=64)
+            vu_codes[b] = results.tile([P, 2 * J], U32, name="vu_codes", align_bytes=64)
+            vu_scales[b] = results.tile([P, 2 * J], U8, name="vu_scales", align_bytes=64)
             nc.vector.quantize_mx(
                 out=vu_codes[b][:].bitcast(FP8X4), scales=vu_scales[b][:], in_=vu[b][:].rearrange("m o n -> m (o n)")
             )
@@ -151,37 +151,35 @@ def tile_block_pb_t_kernel(
                 out=x_biased[b][:], in0=x_in[b][:], in1=proj_b_rows[:].unsqueeze(1).to_broadcast([P, PAR, C]), op=ADD
             )
 
-        def multiply_y(b):
-            y_banks[b] = []
-            for q in range(4):
-                bank = psum.tile([P, K * PAR, QUARTER], F32, name="y_bank%d" % q)
-                y_banks[b].append(bank)
-                for e in range(PAR):
-                    tokens = slice(J + e * P, J + (e + 1) * P)
-                    for k in range(K):
-                        first = k * C + q * QUARTER
-                        nc.tensor.matmul_mx(
-                            out=bank[:, k * PAR + e, :],
-                            lhsT=vu_codes[b][:, tokens].bitcast(FP8X4),
-                            lhsT_scale=vu_scales[b][:, tokens],
-                            rhs=gcn2_words[:, first : first + QUARTER].bitcast(FP8X4),
-                            rhs_scale=w_scales[:, C + first : C + first + QUARTER],
-                            start=True,
-                            stop=True,
-                        )
+        def multiply_y(b, q):
+            bank = psum.tile([P, K * PAR, QUARTER], F32, name="y_bank%d" % q)
+            y_banks[b, q] = bank
+            for e in range(PAR):
+                tokens = slice(J + e * P, J + (e + 1) * P)
+                for k in range(K):
+                    first = k * C + q * QUARTER
+                    nc.tensor.matmul_mx(
+                        out=bank[:, k * PAR + e, :],
+                        lhsT=vu_codes[b][:, tokens].bitcast(FP8X4),
+                        lhsT_scale=vu_scales[b][:, tokens],
+                        rhs=gcn2_words[:, first : first + QUARTER].bitcast(FP8X4),
+                        rhs_scale=w_scales[:, C + first : C + first + QUARTER],
+                        start=True,
+                        stop=True,
+                    )
 
         y_grouped = {}
 
-        def bias_y(b):
-            y_grouped[b] = work.tile([P, 4 * C], BF16, name="y_grouped", align_bytes=64)
-            for q in range(4):
-                part = slice(q * 4 * QUARTER, (q + 1) * 4 * QUARTER)
-                nc.vector.tensor_tensor(
-                    out=y_grouped[b][:, part].rearrange("p (c t) -> p c t", t=4),
-                    in0=y_banks[b][q][:].rearrange("p t c -> p c t"),
-                    in1=y_bias[:, part].rearrange("p (c t) -> p c t", t=4),
-                    op=ADD,
-                )
+        def bias_y(b, q):
+            if q == 0:
+                y_grouped[b] = work.tile([P, 4 * C], BF16, name="y_grouped", align_bytes=64)
+            part = slice(q * 4 * QUARTER, (q + 1) * 4 * QUARTER)
+            nc.vector.tensor_tensor(
+                out=y_grouped[b][:, part].rearrange("p (c t) -> p c t", t=4),
+                in0=y_banks[b, q][:].rearrange("p t c -> p c t"),
+                in1=y_bias[:, part].rearrange("p (c t) -> p c t", t=4),
+                op=ADD,
+            )
 
         def quantise_y(b):
             y_codes[b] = work.tile([P, C], U32, name="y_codes", align_bytes=64)
@@ -233,23 +231,29 @@ def tile_block_pb_t_kernel(
         prepare(1)
         quantise_vu(0)
         combine_v(1)
-        multiply_y(0)
+        prepare(2)
+        for q in range(4):
+            multiply_y(0, q)
+        quantise_vu(1)
         quantise_adj()
         bias_x(0)
-        bias_x(1)
         for b in range(B):
             if b + AHEAD < B:
                 load(b + AHEAD)
-            if b + 2 < B:
-                prepare(b + 2)
-                bias_x(b + 2)
-            bias_y(b)
             if b + 1 < B:
-                quantise_vu(b + 1)
-            quantise_y(b)
+                bias_x(b + 1)
             if b + 2 < B:
                 combine_v(b + 2)
+            if b + 3 < B:
+                prepare(b + 3)
+            for q in range(4):
+                bias_y(b, q)
+                if b + 1 < B:
+                    multiply_y(b + 1, q)
+            quantise_y(b)
+            if b > 0:
+                finish(b - 1)
             multiply_out(b)
-            if b + 1 < B:
-                multiply_y(b + 1)
-            finish(b)
+            if b + 2 < B:
+                quantise_vu(b + 2)
+        finish(B - 1)

@@ -18,7 +18,7 @@ DH = C // H
 S_G2A, S_A2G = 0.5, 0.8
 PAR = J // P
 QUARTER = C // 4
-AHEAD = 4
+AHEAD = 5
 
 FLOPS = 2 * B * J * C * C + 2 * B * J * C * K * C + 2 * B * J * K * J * C
 
@@ -35,13 +35,11 @@ def tile_block_pb_t_kernel(
         psum = ctx.enter_context(tc.psum_pool(name="psum", bufs=1))
         ctx.enter_context(tc.manual_schedule())
 
-        a_in, g_in, x_in = {}, {}, {}
+        a_raw, a_in, g_in, x_in = {}, {}, {}, {}
 
         def load(b):
-            a_in[b] = inputs.tile([P, PAR, C], BF16, name="a_in")
-            by_parity = attn_o[b].rearrange("h (p e) d -> e p h d", e=PAR)
-            for e in range(PAR):
-                nc.sync.dma_start(out=a_in[b][:, e, :].rearrange("p (h d) -> p h d", h=H), in_=by_parity[e])
+            a_raw[b] = inputs.tile([P, H, PAR * DH], BF16, name="a_raw")
+            nc.sync.dma_start(out=a_raw[b][:], in_=attn_o[b].rearrange("h (p e) d -> p h (e d)", e=PAR))
             g_in[b] = inputs.tile([P, PAR, C], BF16, name="g_in")
             nc.sync.dma_start(
                 out=g_in[b][:].rearrange("p e c -> p (e c)"), in_=xg1[b].rearrange("(p e) c -> p (e c)", e=PAR)
@@ -107,6 +105,13 @@ def tile_block_pb_t_kernel(
 
         def by_token(ap):
             return ap.rearrange("m (n s i) -> m n s i", s=2, i=2)
+
+        def sort(b):
+            a_in[b] = work.tile([P, PAR, C], BF16, name="a_in")
+            nc.scalar.copy(
+                out=a_in[b][:].rearrange("p e c -> p (e c)").bitcast(F32).rearrange("p (e h w) -> p e h w", e=PAR, h=H),
+                in_=a_raw[b][:].rearrange("p h c -> p (h c)").bitcast(F32).rearrange("p (h e w) -> p e h w", e=PAR, h=H),
+            )
 
         def transpose(b):
             for name, source, banks in (("a_t", a_in, a_t), ("g_t", g_in, g_t)):
@@ -226,17 +231,21 @@ def tile_block_pb_t_kernel(
             scale(b)
             combine_u(b)
 
+        sort(0)
         prepare(0)
         combine_v(0)
+        sort(1)
         prepare(1)
         quantise_vu(0)
         combine_v(1)
+        sort(2)
         prepare(2)
         for q in range(4):
             multiply_y(0, q)
         quantise_vu(1)
         quantise_adj()
         bias_x(0)
+        sort(3)
         for b in range(B):
             if b + AHEAD < B:
                 load(b + AHEAD)
@@ -246,6 +255,8 @@ def tile_block_pb_t_kernel(
                 combine_v(b + 2)
             if b + 3 < B:
                 prepare(b + 3)
+            if b + 4 < B:
+                sort(b + 4)
             for q in range(4):
                 bias_y(b, q)
                 if b + 1 < B:

@@ -18,7 +18,7 @@ DH = C // H
 S_G2A, S_A2G = 0.5, 0.8
 PAR = J // P
 QUARTER = C // 4
-AHEAD = 5
+AHEAD = 6
 
 FLOPS = 2 * B * J * C * C + 2 * B * J * C * K * C + 2 * B * J * K * J * C
 
@@ -226,45 +226,44 @@ def tile_block_pb_t_kernel(
                 out=out[b].rearrange("(p e) c -> p (e c)", e=PAR), in_=result[:].rearrange("p e c -> p (e c)")
             )
 
-        def prepare(b):
+        for b in range(3):
+            sort(b)
             transpose(b)
             scale(b)
             combine_u(b)
-
-        sort(0)
-        prepare(0)
-        combine_v(0)
-        sort(1)
-        prepare(1)
-        quantise_vu(0)
-        combine_v(1)
-        sort(2)
-        prepare(2)
+            combine_v(b)
+            if b > 0:
+                quantise_vu(b - 1)
         for q in range(4):
             multiply_y(0, q)
-        quantise_vu(1)
+        sort(3)
+        transpose(3)
+        scale(3)
         quantise_adj()
         bias_x(0)
-        sort(3)
+        sort(4)
         for b in range(B):
             if b + AHEAD < B:
                 load(b + AHEAD)
+            if b + 3 < B:
+                combine_u(b + 3)
             if b + 1 < B:
                 bias_x(b + 1)
-            if b + 2 < B:
-                combine_v(b + 2)
             if b + 3 < B:
-                prepare(b + 3)
+                combine_v(b + 3)
+            if b + 5 < B:
+                sort(b + 5)
             if b + 4 < B:
-                sort(b + 4)
+                transpose(b + 4)
+                scale(b + 4)
             for q in range(4):
                 bias_y(b, q)
                 if b + 1 < B:
                     multiply_y(b + 1, q)
-            quantise_y(b)
             if b > 0:
                 finish(b - 1)
-            multiply_out(b)
+            quantise_y(b)
             if b + 2 < B:
                 quantise_vu(b + 2)
+            multiply_out(b)
         finish(B - 1)

@@ -18,7 +18,7 @@ DH = C // H
 S_G2A, S_A2G = 0.5, 0.8
 PAR = J // P
 QUARTER = C // 4
-AHEAD = 6
+AHEAD = 4
 
 FLOPS = 2 * B * J * C * C + 2 * B * J * C * K * C + 2 * B * J * K * J * C
 
@@ -37,13 +37,15 @@ def tile_block_pb_t_kernel(
 
         a_raw, a_in, g_in, x_in = {}, {}, {}, {}
 
-        def load(b):
+        def load_streams(b):
             a_raw[b] = inputs.tile([P, H, PAR * DH], BF16, name="a_raw")
             nc.sync.dma_start(out=a_raw[b][:], in_=attn_o[b].rearrange("h (p e) d -> p h (e d)", e=PAR))
             g_in[b] = inputs.tile([P, PAR, C], BF16, name="g_in")
             nc.sync.dma_start(
                 out=g_in[b][:].rearrange("p e c -> p (e c)"), in_=xg1[b].rearrange("(p e) c -> p (e c)", e=PAR)
             )
+
+        def load_x(b):
             x_in[b] = inputs.tile([P, PAR, C], BF16, name="x_in")
             nc.sync.dma_start(
                 out=x_in[b][:].rearrange("p e c -> p (e c)"), in_=x[b].rearrange("(p e) c -> p (e c)", e=PAR)
@@ -51,39 +53,44 @@ def tile_block_pb_t_kernel(
 
         w_scales = const.tile([P, C + K * C], U8, align_bytes=64)
         nc.vector.memset(w_scales[:].bitcast(I32), 0)
-        load(0)
-        for r in range(4):
-            nc.sync.dma_start(out=w_scales[r:P:32, C:].bitcast(I32), in_=gcn2_w_scales[0, r:16:4, :].bitcast(I32))
-        for r in range(4):
-            nc.sync.dma_start(out=w_scales[r:P:32, :C].bitcast(I32), in_=proj_w_scales[0, r:16:4, :].bitcast(I32))
+        identity = const.tile([P, P], F32)
+        make_identity(nc, identity[:])
+
+        load_streams(0)
         gcn2_words = const.tile([P, K * C], U32, align_bytes=64)
         nc.sync.dma_start(
             out=gcn2_words[:].bitcast(I32), in_=gcn2_w_words[0].rearrange("p n t -> p (n t)").bitcast(I32)
         )
+        for r in range(4):
+            nc.sync.dma_start(out=w_scales[r:P:32, C:].bitcast(I32), in_=gcn2_w_scales[0, r:16:4, :].bitcast(I32))
+        gcn2_b_rows = const.tile([P, K * C], BF16)
+        nc.sync.dma_start(out=gcn2_b_rows[:], in_=gcn2_b.partition_broadcast(P))
+        load_streams(1)
         proj_words = const.tile([P, C], U32, align_bytes=64)
         nc.sync.dma_start(
             out=proj_words[:].bitcast(I32), in_=proj_w_words[0].rearrange("p n t -> p (n t)").bitcast(I32)
         )
+        for r in range(4):
+            nc.sync.dma_start(out=w_scales[r:P:32, :C].bitcast(I32), in_=proj_w_scales[0, r:16:4, :].bitcast(I32))
         adj_raw = const.tile([P, K * PAR, J], BF16)
         nc.sync.dma_start(
             out=adj_raw[:].rearrange("p (k e) w -> p k (e w)", k=K), in_=adj.rearrange("k (p e) w -> p k (e w)", e=PAR)
         )
-        for b in range(1, AHEAD):
-            load(b)
-
-        gcn2_b_rows = const.tile([P, K * C], BF16)
-        nc.scalar.dma_start(out=gcn2_b_rows[:], in_=gcn2_b.partition_broadcast(P))
         proj_b_rows = const.tile([P, C], BF16)
-        nc.scalar.dma_start(out=proj_b_rows[:], in_=proj_b.partition_broadcast(P))
-
-        identity = const.tile([P, P], F32)
-        make_identity(nc, identity[:])
+        nc.sync.dma_start(out=proj_b_rows[:], in_=proj_b.partition_broadcast(P))
+        load_x(0)
+        for b in range(2, AHEAD):
+            load_streams(b)
+        for b in range(1, AHEAD):
+            load_x(b)
 
         y_bias = const.tile([P, C * K * PAR], BF16)
-        nc.vector.tensor_copy(
-            out=y_bias[:].rearrange("p (c k e) -> p c k e", k=K, e=PAR),
-            in_=gcn2_b_rows[:].rearrange("p (k c) -> p c k", k=K).unsqueeze(3).to_broadcast([P, C, K, PAR]),
-        )
+
+        def spread_y_bias():
+            nc.vector.tensor_copy(
+                out=y_bias[:].rearrange("p (c k e) -> p c k e", k=K, e=PAR),
+                in_=gcn2_b_rows[:].rearrange("p (k c) -> p c k", k=K).unsqueeze(3).to_broadcast([P, C, K, PAR]),
+            )
 
         adj_codes = const.tile([P, J], U32, align_bytes=64)
         adj_scales = const.tile([P, J], U8, align_bytes=64)
@@ -140,7 +147,7 @@ def tile_block_pb_t_kernel(
             )
 
         def combine_u(b):
-            vu[b] = work.tile([P, 2, 4 * J], BF16, name="vu", align_bytes=64)
+            vu[b] = const.tile([P, 2, 4 * J], BF16, name="vu", align_bytes=64)
             nc.gpsimd.tensor_tensor(out=vu[b][:, 1, :], in0=g_plain[b][:], in1=a_scaled[b][:], op=ADD)
 
         def quantise_vu(b):
@@ -220,50 +227,52 @@ def tile_block_pb_t_kernel(
 
         def finish(b):
             result = results.tile([P, PAR, C], F32, name="result")
+            by_parity = out[b].rearrange("(p e) c -> e p c", e=PAR)
             for f in range(PAR):
                 nc.vector.tensor_tensor(out=result[:, f, :], in0=out_banks[b][f][:], in1=x_biased[b][:, f, :], op=ADD)
-            nc.sync.dma_start(
-                out=out[b].rearrange("(p e) c -> p (e c)", e=PAR), in_=result[:].rearrange("p e c -> p (e c)")
-            )
+                nc.sync.dma_start(out=by_parity[f], in_=result[:, f, :])
 
-        for b in range(3):
-            sort(b)
-            transpose(b)
-            scale(b)
-            combine_u(b)
-            combine_v(b)
-            if b > 0:
-                quantise_vu(b - 1)
+        sort(0)
+        transpose(0)
+        scale(0)
+        combine_u(0)
+        combine_v(0)
+        quantise_vu(0)
+        spread_y_bias()
+        sort(1)
+        transpose(1)
+        scale(1)
+        combine_u(1)
         for q in range(4):
             multiply_y(0, q)
-        sort(3)
-        transpose(3)
-        scale(3)
-        quantise_adj()
         bias_x(0)
-        sort(4)
+        sort(2)
+        quantise_adj()
         for b in range(B):
             if b + AHEAD < B:
-                load(b + AHEAD)
+                load_streams(b + AHEAD)
+                load_x(b + AHEAD)
+            bias_y(b, 0)
+            bias_y(b, 1)
+            if b + 1 < B:
+                combine_v(b + 1)
+            if b + 2 < B:
+                transpose(b + 2)
+                scale(b + 2)
             if b + 3 < B:
-                combine_u(b + 3)
+                sort(b + 3)
+            bias_y(b, 2)
+            bias_y(b, 3)
+            if b + 1 < B:
+                quantise_vu(b + 1)
+            quantise_y(b)
+            if b + 2 < B:
+                combine_u(b + 2)
             if b + 1 < B:
                 bias_x(b + 1)
-            if b + 3 < B:
-                combine_v(b + 3)
-            if b + 5 < B:
-                sort(b + 5)
-            if b + 4 < B:
-                transpose(b + 4)
-                scale(b + 4)
-            for q in range(4):
-                bias_y(b, q)
-                if b + 1 < B:
+                for q in range(4):
                     multiply_y(b + 1, q)
             if b > 0:
                 finish(b - 1)
-            quantise_y(b)
-            if b + 2 < B:
-                quantise_vu(b + 2)
             multiply_out(b)
         finish(B - 1)

@@ -253,7 +253,6 @@ def tile_block_pb_t_kernel(
                 load_streams(b + AHEAD)
                 load_x(b + AHEAD)
             bias_y(b, 0)
-            bias_y(b, 1)
             if b + 1 < B:
                 combine_v(b + 1)
             if b + 2 < B:
@@ -261,6 +260,7 @@ def tile_block_pb_t_kernel(
                 scale(b + 2)
             if b + 3 < B:
                 sort(b + 3)
+            bias_y(b, 1)
             bias_y(b, 2)
             bias_y(b, 3)
             if b + 1 < B:

@@ -11,13 +11,15 @@ U8 = mybir.dt.uint8
 FP8X4 = mybir.dt.float8_e4m3fn_x4
 ADD = mybir.AluOpType.add
 COPY = mybir.ActivationFunctionType.Copy
+IDENTITY = mybir.ActivationFunctionType.Identity
 
 P = 128
 B, J, C, K, H = 16, 256, 512, 2, 8
 DH = C // H
 S_G2A, S_A2G = 0.5, 0.8
 PAR = J // P
-QUARTER = C // 4
+QUARTERS = C // P
+PACK = 4
 AHEAD = 4
 
 FLOPS = 2 * B * J * C * C + 2 * B * J * C * K * C + 2 * B * J * K * J * C
@@ -32,14 +34,17 @@ def tile_block_pb_t_kernel(
         inputs = ctx.enter_context(tc.tile_pool(name="inputs", bufs=AHEAD))
         work = ctx.enter_context(tc.tile_pool(name="work", bufs=2))
         results = ctx.enter_context(tc.tile_pool(name="results", bufs=3))
+        ring = ctx.enter_context(tc.tile_pool(name="ring", bufs=5))
         psum = ctx.enter_context(tc.psum_pool(name="psum", bufs=1))
         ctx.enter_context(tc.manual_schedule())
 
-        a_raw, a_in, g_in, x_in = {}, {}, {}, {}
+        a_in, g_in, x_in = {}, {}, {}
 
         def load_streams(b):
-            a_raw[b] = inputs.tile([P, H, PAR * DH], BF16, name="a_raw")
-            nc.sync.dma_start(out=a_raw[b][:], in_=attn_o[b].rearrange("h (p e) d -> p h (e d)", e=PAR))
+            a_in[b] = inputs.tile([P, PAR, C], BF16, name="a_in")
+            by_parity = attn_o[b].rearrange("h (p e) d -> e p h d", e=PAR)
+            for e in range(PAR):
+                nc.sync.dma_start(out=a_in[b][:, e, :].rearrange("p (h d) -> p h d", h=H), in_=by_parity[e])
             g_in[b] = inputs.tile([P, PAR, C], BF16, name="g_in")
             nc.sync.dma_start(
                 out=g_in[b][:].rearrange("p e c -> p (e c)"), in_=xg1[b].rearrange("(p e) c -> p (e c)", e=PAR)
@@ -53,6 +58,8 @@ def tile_block_pb_t_kernel(
 
         w_scales = const.tile([P, C + K * C], U8, align_bytes=64)
         nc.vector.memset(w_scales[:].bitcast(I32), 0)
+        gcn2_b_rows = const.tile([P, P], BF16)
+        nc.vector.memset(gcn2_b_rows[:], 0.0)
         identity = const.tile([P, P], F32)
         make_identity(nc, identity[:])
 
@@ -63,8 +70,7 @@ def tile_block_pb_t_kernel(
         )
         for r in range(4):
             nc.sync.dma_start(out=w_scales[r:P:32, C:].bitcast(I32), in_=gcn2_w_scales[0, r:16:4, :].bitcast(I32))
-        gcn2_b_rows = const.tile([P, K * C], BF16)
-        nc.sync.dma_start(out=gcn2_b_rows[:], in_=gcn2_b.partition_broadcast(P))
+        nc.sync.dma_start(out=gcn2_b_rows[: K * QUARTERS, :], in_=gcn2_b.rearrange("(r n) -> r n", n=P))
         load_streams(1)
         proj_words = const.tile([P, C], U32, align_bytes=64)
         nc.sync.dma_start(
@@ -72,39 +78,42 @@ def tile_block_pb_t_kernel(
         )
         for r in range(4):
             nc.sync.dma_start(out=w_scales[r:P:32, :C].bitcast(I32), in_=proj_w_scales[0, r:16:4, :].bitcast(I32))
-        adj_raw = const.tile([P, K * PAR, J], BF16)
+        adj_raw = const.tile([P, PACK, J], BF16)
         nc.sync.dma_start(
-            out=adj_raw[:].rearrange("p (k e) w -> p k (e w)", k=K), in_=adj.rearrange("k (p e) w -> p k (e w)", e=PAR)
+            out=adj_raw[:].rearrange("p t w -> p (t w)"),
+            in_=adj.rearrange("k j w -> (k j) w").rearrange("(p t) w -> p (t w)", t=PACK),
         )
         proj_b_rows = const.tile([P, C], BF16)
         nc.sync.dma_start(out=proj_b_rows[:], in_=proj_b.partition_broadcast(P))
         load_x(0)
+        load_x(1)
         for b in range(2, AHEAD):
             load_streams(b)
-        for b in range(1, AHEAD):
             load_x(b)
 
-        y_bias = const.tile([P, C * K * PAR], BF16)
+        y_bias = const.tile([P, K * QUARTERS], F32)
 
-        def spread_y_bias():
-            nc.vector.tensor_copy(
-                out=y_bias[:].rearrange("p (c k e) -> p c k e", k=K, e=PAR),
-                in_=gcn2_b_rows[:].rearrange("p (k c) -> p c k", k=K).unsqueeze(3).to_broadcast([P, C, K, PAR]),
-            )
+        def make_y_bias():
+            rows = const.tile([P, P], F32)
+            nc.vector.tensor_copy(out=rows[:], in_=gcn2_b_rows[:])
+            columns = psum.tile([P, P], F32, name="y_bank0")
+            nc.tensor.transpose(columns[:], rows[:], identity[:])
+            nc.scalar.copy(out=y_bias[:], in_=columns[:, : K * QUARTERS])
 
         adj_codes = const.tile([P, J], U32, align_bytes=64)
         adj_scales = const.tile([P, J], U8, align_bytes=64)
 
         def quantise_adj():
-            adj_grouped = const.tile([P, J * K * PAR], BF16, align_bytes=64)
+            adj_grouped = const.tile([P, J * PACK], BF16, align_bytes=64)
             nc.vector.tensor_copy(
-                out=adj_grouped[:].rearrange("p (f m t) -> p f m t", f=PAR, t=K * PAR),
+                out=adj_grouped[:].rearrange("p (f m t) -> p f m t", f=PAR, t=PACK),
                 in_=adj_raw[:].rearrange("p t (m f) -> p f m t", f=PAR),
             )
             nc.vector.quantize_mx(out=adj_codes[:].bitcast(FP8X4), scales=adj_scales[:], in_=adj_grouped[:])
 
-        a_t, g_t, a_scaled, g_scaled, g_plain, vu, vu_codes, vu_scales = {}, {}, {}, {}, {}, {}, {}, {}
-        y_banks, y_codes, y_scales, x_biased = {}, {}, {}, {}
+        a_t, g_t, a_scaled, g_plain, g_half, vu, vu_codes, vu_scales = {}, {}, {}, {}, {}, {}, {}, {}
+        y_t_banks, y_t, y_banks, y_grouped, y_codes, y_scales = {}, {}, {}, {}, {}, {}
+        out_banks, x_biased, result = {}, {}, {}
 
         def pairs_by_token(bank):
             halves = bank[:].rearrange("m s n -> m (s n)").bitcast(BF16)
@@ -113,42 +122,47 @@ def tile_block_pb_t_kernel(
         def by_token(ap):
             return ap.rearrange("m (n s i) -> m n s i", s=2, i=2)
 
-        def sort(b):
-            a_in[b] = work.tile([P, PAR, C], BF16, name="a_in")
-            nc.scalar.copy(
-                out=a_in[b][:].rearrange("p e c -> p (e c)").bitcast(F32).rearrange("p (e h w) -> p e h w", e=PAR, h=H),
-                in_=a_raw[b][:].rearrange("p h c -> p (h c)").bitcast(F32).rearrange("p (h e w) -> p e h w", e=PAR, h=H),
-            )
+        def transpose_stream(source, bank):
+            words = source[:].rearrange("p e c -> p (e c)").bitcast(F32)
+            for e in range(PAR):
+                for s in range(2):
+                    first = e * (C // 2) + s
+                    nc.tensor.transpose(
+                        bank[:, s, e * P : (e + 1) * P], words[:, first : (e + 1) * (C // 2) : 2], identity[:]
+                    )
 
-        def transpose(b):
-            for name, source, banks in (("a_t", a_in, a_t), ("g_t", g_in, g_t)):
-                banks[b] = psum.tile([P, 2, J], F32, name=name)
-                words = source[b][:].rearrange("p e c -> p (e c)").bitcast(F32)
-                for e in range(PAR):
-                    for s in range(2):
-                        first = e * (C // 2) + s
-                        nc.tensor.transpose(
-                            banks[b][:, s, e * P : (e + 1) * P], words[:, first : (e + 1) * (C // 2) : 2], identity[:]
-                        )
+        def transpose_a(b):
+            a_t[b] = psum.tile([P, 2, J], F32, name="a_t")
+            transpose_stream(a_in[b], a_t[b])
 
-        def scale(b):
+        def transpose_g(b):
+            g_t[b] = psum.tile([P, 2, J], F32, name="g_t")
+            transpose_stream(g_in[b], g_t[b])
+
+        def scale_a(b):
             a_scaled[b] = work.tile([P, 4 * J], F32, name="a_scaled")
             nc.scalar.activation(out=by_token(a_scaled[b][:]), in_=pairs_by_token(a_t[b]), func=COPY, scale=S_A2G)
-            g_plain[b] = work.tile([P, 4 * J], BF16, name="g_plain")
+
+        def copy_g(b):
+            g_plain[b] = ring.tile([P, 4 * J], BF16, name="g_plain", tag="ring")
             nc.scalar.copy(
                 out=g_plain[b][:].bitcast(F32).rearrange("m (n s) -> m n s", s=2), in_=g_t[b][:].rearrange("m s n -> m n s")
             )
-            g_scaled[b] = work.tile([P, 4 * J], BF16, name="g_scaled")
-            nc.scalar.activation(out=by_token(g_scaled[b][:]), in_=pairs_by_token(g_t[b]), func=COPY, scale=S_G2A)
+
+        def halve_g(b):
+            g_half[b] = work.tile([P, 4 * J], BF16, name="g_half")
+            nc.vector.tensor_scalar_mul(g_half[b][:], g_plain[b][:], S_G2A)
+
+        def combine_u(b):
+            vu[b] = work.tile([P, 2, 4 * J], BF16, name="vu", align_bytes=64)
+            nc.vector.tensor_tensor(
+                out=by_token(vu[b][:, 1, :]), in0=pairs_by_token(g_t[b]), in1=by_token(a_scaled[b][:]), op=ADD
+            )
 
         def combine_v(b):
             nc.vector.tensor_tensor(
-                out=by_token(vu[b][:, 0, :]), in0=pairs_by_token(a_t[b]), in1=by_token(g_scaled[b][:]), op=ADD
+                out=by_token(vu[b][:, 0, :]), in0=pairs_by_token(a_t[b]), in1=by_token(g_half[b][:]), op=ADD
             )
-
-        def combine_u(b):
-            vu[b] = const.tile([P, 2, 4 * J], BF16, name="vu", align_bytes=64)
-            nc.gpsimd.tensor_tensor(out=vu[b][:, 1, :], in0=g_plain[b][:], in1=a_scaled[b][:], op=ADD)
 
         def quantise_vu(b):
             vu_codes[b] = results.tile([P, 2 * J], U32, name="vu_codes", align_bytes=64)
@@ -158,121 +172,131 @@ def tile_block_pb_t_kernel(
             )
 
         def bias_x(b):
-            x_biased[b] = results.tile([P, PAR, C], F32, name="x_biased")
+            x_biased[b] = ring.tile([P, PAR, C], F32, name="x_biased", tag="ring")
             nc.gpsimd.tensor_tensor(
                 out=x_biased[b][:], in0=x_in[b][:], in1=proj_b_rows[:].unsqueeze(1).to_broadcast([P, PAR, C]), op=ADD
             )
 
         def multiply_y(b, q):
-            bank = psum.tile([P, K * PAR, QUARTER], F32, name="y_bank%d" % q)
-            y_banks[b, q] = bank
-            for e in range(PAR):
-                tokens = slice(J + e * P, J + (e + 1) * P)
-                for k in range(K):
-                    first = k * C + q * QUARTER
-                    nc.tensor.matmul_mx(
-                        out=bank[:, k * PAR + e, :],
-                        lhsT=vu_codes[b][:, tokens].bitcast(FP8X4),
-                        lhsT_scale=vu_scales[b][:, tokens],
-                        rhs=gcn2_words[:, first : first + QUARTER].bitcast(FP8X4),
-                        rhs_scale=w_scales[:, C + first : C + first + QUARTER],
-                        start=True,
-                        stop=True,
-                    )
-
-        y_grouped = {}
+            bank = psum.tile([P, K, J], F32, name="y_t_bank%d" % (q % 2))
+            y_t_banks[b, q] = bank
+            for k in range(K):
+                first = k * C + q * P
+                nc.tensor.matmul_mx(
+                    out=bank[:, k, :],
+                    lhsT=gcn2_words[:, first : first + P].bitcast(FP8X4),
+                    lhsT_scale=w_scales[:, C + first : C + first + P],
+                    rhs=vu_codes[b][:, J:].bitcast(FP8X4),
+                    rhs_scale=vu_scales[b][:, J:],
+                    start=True,
+                    stop=True,
+                )
 
         def bias_y(b, q):
             if q == 0:
-                y_grouped[b] = work.tile([P, 4 * C], BF16, name="y_grouped", align_bytes=64)
-            part = slice(q * 4 * QUARTER, (q + 1) * 4 * QUARTER)
-            nc.vector.tensor_tensor(
-                out=y_grouped[b][:, part].rearrange("p (c t) -> p c t", t=4),
-                in0=y_banks[b, q][:].rearrange("p t c -> p c t"),
-                in1=y_bias[:, part].rearrange("p (c t) -> p c t", t=4),
-                op=ADD,
-            )
+                y_t[b] = work.tile([P, QUARTERS, 2, K, J // 2], BF16, name="y_t")
+            for k in range(K):
+                laid_out = y_t[b][:, q, :, k, :].rearrange("m s (w e) -> m s w e", e=PAR)
+                joints = y_t_banks[b, q][:, k, :].rearrange("m (e w s) -> m s w e", e=PAR, s=2)
+                column = y_bias[:, k * QUARTERS + q : k * QUARTERS + q + 1]
+                if b == B - 1 and q % 2 == 1:
+                    nc.vector.tensor_scalar(out=laid_out, in0=joints, scalar1=column, scalar2=None, op0=ADD)
+                else:
+                    nc.scalar.activation(out=laid_out, in_=joints, func=IDENTITY, bias=column)
+
+        def transpose_y(b, half):
+            bank = psum.tile([P, 2, 2, P], F32, name="y_bank%d" % half)
+            y_banks[b, half] = bank
+            for i in range(2):
+                words = y_t[b][:, 2 * half + i].rearrange("m s k n -> m (s k n)").bitcast(F32)
+                for s in range(2):
+                    nc.tensor.transpose(bank[:, i, s, :], words[:, s * P : (s + 1) * P], identity[:])
+
+        def group_y(b, half):
+            if half == 0:
+                y_grouped[b] = work.tile([P, PACK * C], BF16, name="y_grouped", align_bytes=64)
+            part = slice(half * PACK * C // 2, (half + 1) * PACK * C // 2)
+            words = y_grouped[b][:, part].bitcast(F32).rearrange("p (i c s) -> p i c s", i=2, s=2)
+            source = y_banks[b, half][:].rearrange("p i s c -> p i c s")
+            if half == 0:
+                nc.vector.tensor_copy(out=words, in_=source)
+            else:
+                nc.scalar.copy(out=words, in_=source)
 
         def quantise_y(b):
             y_codes[b] = work.tile([P, C], U32, name="y_codes", align_bytes=64)
             y_scales[b] = work.tile([P, C], U8, name="y_scales", align_bytes=64)
             nc.vector.quantize_mx(out=y_codes[b][:].bitcast(FP8X4), scales=y_scales[b][:], in_=y_grouped[b][:])
 
-        out_banks = {}
+        def multiply_out(b, f):
+            bank = psum.tile([P, C], F32, name="out_bank%d" % f)
+            out_banks[b, f] = bank
+            tokens = slice(f * P, (f + 1) * P)
+            nc.tensor.matmul_mx(
+                out=bank[:],
+                lhsT=vu_codes[b][:, tokens].bitcast(FP8X4),
+                lhsT_scale=vu_scales[b][:, tokens],
+                rhs=proj_words[:].bitcast(FP8X4),
+                rhs_scale=w_scales[:, :C],
+                start=True,
+                stop=False,
+            )
+            nc.tensor.matmul_mx(
+                out=bank[:],
+                lhsT=adj_codes[:, tokens].bitcast(FP8X4),
+                lhsT_scale=adj_scales[:, tokens],
+                rhs=y_codes[b][:].bitcast(FP8X4),
+                rhs_scale=y_scales[b][:],
+                start=False,
+                stop=True,
+            )
 
-        def multiply_out(b):
-            out_banks[b] = []
-            for f in range(PAR):
-                bank = psum.tile([P, C], F32, name="out_bank%d" % f)
-                out_banks[b].append(bank)
-                tokens = slice(f * P, (f + 1) * P)
-                nc.tensor.matmul_mx(
-                    out=bank[:],
-                    lhsT=vu_codes[b][:, tokens].bitcast(FP8X4),
-                    lhsT_scale=vu_scales[b][:, tokens],
-                    rhs=proj_words[:].bitcast(FP8X4),
-                    rhs_scale=w_scales[:, :C],
-                    start=True,
-                    stop=False,
-                )
-                nc.tensor.matmul_mx(
-                    out=bank[:],
-                    lhsT=adj_codes[:, tokens].bitcast(FP8X4),
-                    lhsT_scale=adj_scales[:, tokens],
-                    rhs=y_codes[b][:].bitcast(FP8X4),
-                    rhs_scale=y_scales[b][:],
-                    start=False,
-                    stop=True,
-                )
+        def finish(b, f):
+            if f == 0:
+                result[b] = results.tile([P, PAR, C], F32, name="result")
+            nc.vector.tensor_tensor(
+                out=result[b][:, f, :], in0=out_banks[b, f][:], in1=x_biased[b][:, f, :], op=ADD
+            )
+            nc.sync.dma_start(out=out[b].rearrange("(p e) c -> e p c", e=PAR)[f], in_=result[b][:, f, :])
 
-        def finish(b):
-            result = results.tile([P, PAR, C], F32, name="result")
-            by_parity = out[b].rearrange("(p e) c -> e p c", e=PAR)
-            for f in range(PAR):
-                nc.vector.tensor_tensor(out=result[:, f, :], in0=out_banks[b][f][:], in1=x_biased[b][:, f, :], op=ADD)
-                nc.sync.dma_start(out=by_parity[f], in_=result[:, f, :])
+        def when(stage, b, *rest):
+            if 0 <= b < B:
+                stage(b, *rest)
 
-        sort(0)
-        transpose(0)
-        scale(0)
-        combine_u(0)
-        combine_v(0)
-        quantise_vu(0)
-        spread_y_bias()
-        sort(1)
-        transpose(1)
-        scale(1)
-        combine_u(1)
-        for q in range(4):
-            multiply_y(0, q)
-        bias_x(0)
-        sort(2)
-        quantise_adj()
-        for b in range(B):
-            if b + AHEAD < B:
-                load_streams(b + AHEAD)
-                load_x(b + AHEAD)
-            bias_y(b, 0)
-            if b + 1 < B:
-                combine_v(b + 1)
-            if b + 2 < B:
-                transpose(b + 2)
-                scale(b + 2)
-            if b + 3 < B:
-                sort(b + 3)
-            bias_y(b, 1)
-            bias_y(b, 2)
-            bias_y(b, 3)
-            if b + 1 < B:
-                quantise_vu(b + 1)
-            quantise_y(b)
-            if b + 2 < B:
-                combine_u(b + 2)
-            if b + 1 < B:
-                bias_x(b + 1)
-                for q in range(4):
-                    multiply_y(b + 1, q)
-            if b > 0:
-                finish(b - 1)
-            multiply_out(b)
-        finish(B - 1)
+        def load_next(b):
+            if AHEAD <= b:
+                load_streams(b)
+                load_x(b)
+
+        for r in range(-2, B + 1):
+            when(multiply_y, r, 0)
+            when(multiply_y, r, 1)
+            when(bias_y, r, 0)
+            when(bias_y, r, 1)
+            when(combine_u, r + 1)
+            when(bias_x, r + 2)
+            when(multiply_out, r - 1, 0)
+            when(multiply_y, r, 2)
+            when(bias_y, r, 2)
+            when(finish, r - 1, 0)
+            when(multiply_out, r - 1, 1)
+            when(multiply_y, r, 3)
+            when(bias_y, r, 3)
+            when(combine_v, r + 1)
+            when(finish, r - 1, 1)
+            when(transpose_g, r + 2)
+            when(copy_g, r + 2)
+            when(transpose_y, r, 0)
+            when(transpose_y, r, 1)
+            when(group_y, r, 0)
+            when(group_y, r, 1)
+            when(transpose_a, r + 2)
+            when(scale_a, r + 2)
+            when(load_next, r + 2 + AHEAD)
+            when(quantise_vu, r + 1)
+            if r == -1:
+                make_y_bias()
+            if r == 0:
+                quantise_adj()
+            when(halve_g, r + 2)
+            when(quantise_y, r)

@@ -79,10 +79,12 @@ def tile_block_pb_t_kernel(
         for r in range(4):
             nc.sync.dma_start(out=w_scales[r:P:32, :C].bitcast(I32), in_=proj_w_scales[0, r:16:4, :].bitcast(I32))
         adj_raw = const.tile([P, PACK, J], BF16)
-        nc.sync.dma_start(
-            out=adj_raw[:].rearrange("p t w -> p (t w)"),
-            in_=adj.rearrange("k j w -> (k j) w").rearrange("(p t) w -> p (t w)", t=PACK),
-        )
+        for e in range(PAR):
+            for k in range(K):
+                nc.sync.dma_start(
+                    out=adj_raw[e * P // 2 : (e + 1) * P // 2, 2 * k : 2 * k + 2, :],
+                    in_=adj[k].rearrange("(m i e) w -> e m i w", i=2, e=PAR)[e],
+                )
         proj_b_rows = const.tile([P, C], BF16)
         nc.sync.dma_start(out=proj_b_rows[:], in_=proj_b.partition_broadcast(P))
         load_x(0)
@@ -194,10 +196,10 @@ def tile_block_pb_t_kernel(
 
         def bias_y(b, q):
             if q == 0:
-                y_t[b] = work.tile([P, QUARTERS, 2, K, J // 2], BF16, name="y_t")
+                y_t[b] = work.tile([P, QUARTERS, K, J], BF16, name="y_t")
             for k in range(K):
-                laid_out = y_t[b][:, q, :, k, :].rearrange("m s (w e) -> m s w e", e=PAR)
-                joints = y_t_banks[b, q][:, k, :].rearrange("m (e w s) -> m s w e", e=PAR, s=2)
+                laid_out = y_t[b][:, q, k, :]
+                joints = y_t_banks[b, q][:, k, :]
                 column = y_bias[:, k * QUARTERS + q : k * QUARTERS + q + 1]
                 if b == B - 1 and q % 2 == 1:
                     nc.vector.tensor_scalar(out=laid_out, in0=joints, scalar1=column, scalar2=None, op0=ADD)
@@ -205,19 +207,18 @@ def tile_block_pb_t_kernel(
                     nc.scalar.activation(out=laid_out, in_=joints, func=IDENTITY, bias=column)
 
         def transpose_y(b, half):
-            bank = psum.tile([P, 2, 2, P], F32, name="y_bank%d" % half)
+            bank = psum.tile([P, 2, K, P], F32, name="y_bank%d" % half)
             y_banks[b, half] = bank
             for i in range(2):
-                words = y_t[b][:, 2 * half + i].rearrange("m s k n -> m (s k n)").bitcast(F32)
-                for s in range(2):
-                    nc.tensor.transpose(bank[:, i, s, :], words[:, s * P : (s + 1) * P], identity[:])
+                for k in range(K):
+                    nc.tensor.transpose(bank[:, i, k, :], y_t[b][:, 2 * half + i, k, :].bitcast(F32), identity[:])
 
         def group_y(b, half):
             if half == 0:
                 y_grouped[b] = work.tile([P, PACK * C], BF16, name="y_grouped", align_bytes=64)
             part = slice(half * PACK * C // 2, (half + 1) * PACK * C // 2)
-            words = y_grouped[b][:, part].bitcast(F32).rearrange("p (i c s) -> p i c s", i=2, s=2)
-            source = y_banks[b, half][:].rearrange("p i s c -> p i c s")
+            words = y_grouped[b][:, part].bitcast(F32).rearrange("p (i c k) -> p i c k", i=2, k=K)
+            source = y_banks[b, half][:].rearrange("p i k c -> p i c k")
             if half == 0:
                 nc.vector.tensor_copy(out=words, in_=source)
             else:

@@ -34,7 +34,6 @@ def tile_block_pb_t_kernel(
         inputs = ctx.enter_context(tc.tile_pool(name="inputs", bufs=AHEAD))
         work = ctx.enter_context(tc.tile_pool(name="work", bufs=2))
         results = ctx.enter_context(tc.tile_pool(name="results", bufs=3))
-        ring = ctx.enter_context(tc.tile_pool(name="ring", bufs=5))
         psum = ctx.enter_context(tc.psum_pool(name="psum", bufs=1))
         ctx.enter_context(tc.manual_schedule())
 
@@ -146,7 +145,7 @@ def tile_block_pb_t_kernel(
             nc.scalar.activation(out=by_token(a_scaled[b][:]), in_=pairs_by_token(a_t[b]), func=COPY, scale=S_A2G)
 
         def copy_g(b):
-            g_plain[b] = ring.tile([P, 4 * J], BF16, name="g_plain", tag="ring")
+            g_plain[b] = work.tile([P, 4 * J], BF16, name="g_plain")
             nc.scalar.copy(
                 out=g_plain[b][:].bitcast(F32).rearrange("m (n s) -> m n s", s=2), in_=g_t[b][:].rearrange("m s n -> m n s")
             )
@@ -174,8 +173,8 @@ def tile_block_pb_t_kernel(
             )
 
         def bias_x(b):
-            x_biased[b] = ring.tile([P, PAR, C], F32, name="x_biased", tag="ring")
-            nc.gpsimd.tensor_tensor(
+            x_biased[b] = results.tile([P, PAR, C], F32, name="x_biased")
+            nc.vector.tensor_tensor(
                 out=x_biased[b][:], in0=x_in[b][:], in1=proj_b_rows[:].unsqueeze(1).to_broadcast([P, PAR, C]), op=ADD
             )
 
@@ -219,10 +218,7 @@ def tile_block_pb_t_kernel(
             part = slice(half * PACK * C // 2, (half + 1) * PACK * C // 2)
             words = y_grouped[b][:, part].bitcast(F32).rearrange("p (i c k) -> p i c k", i=2, k=K)
             source = y_banks[b, half][:].rearrange("p i k c -> p i c k")
-            if half == 0:
-                nc.vector.tensor_copy(out=words, in_=source)
-            else:
-                nc.scalar.copy(out=words, in_=source)
+            nc.scalar.copy(out=words, in_=source)
 
         def quantise_y(b):
             y_codes[b] = work.tile([P, C], U32, name="y_codes", align_bytes=64)
@@ -275,7 +271,6 @@ def tile_block_pb_t_kernel(
             when(bias_y, r, 0)
             when(bias_y, r, 1)
             when(combine_u, r + 1)
-            when(bias_x, r + 2)
             when(multiply_out, r - 1, 0)
             when(multiply_y, r, 2)
             when(bias_y, r, 2)
@@ -300,4 +295,5 @@ def tile_block_pb_t_kernel(
             if r == 0:
                 quantise_adj()
             when(halve_g, r + 2)
+            when(bias_x, r)
             when(quantise_y, r)

@@ -10,7 +10,7 @@ U32 = mybir.dt.uint32
 U8 = mybir.dt.uint8
 FP8X4 = mybir.dt.float8_e4m3fn_x4
 ADD = mybir.AluOpType.add
-COPY = mybir.ActivationFunctionType.Copy
+MULT = mybir.AluOpType.mult
 IDENTITY = mybir.ActivationFunctionType.Identity
 
 P = 128
@@ -40,10 +40,10 @@ def tile_block_pb_t_kernel(
         a_in, g_in, x_in = {}, {}, {}
 
         def load_streams(b):
-            a_in[b] = inputs.tile([P, PAR, C], BF16, name="a_in")
-            by_parity = attn_o[b].rearrange("h (p e) d -> e p h d", e=PAR)
-            for e in range(PAR):
-                nc.sync.dma_start(out=a_in[b][:, e, :].rearrange("p (h d) -> p h d", h=H), in_=by_parity[e])
+            a_in[b] = inputs.tile([P, H, PAR, DH], BF16, name="a_in")
+            nc.sync.dma_start(
+                out=a_in[b][:].rearrange("p h e d -> p h (e d)"), in_=attn_o[b].rearrange("h (p e) d -> p h (e d)", e=PAR)
+            )
             g_in[b] = inputs.tile([P, PAR, C], BF16, name="g_in")
             nc.sync.dma_start(
                 out=g_in[b][:].rearrange("p e c -> p (e c)"), in_=xg1[b].rearrange("(p e) c -> p (e c)", e=PAR)
@@ -63,6 +63,7 @@ def tile_block_pb_t_kernel(
         make_identity(nc, identity[:])
 
         load_streams(0)
+        load_streams(1)
         gcn2_words = const.tile([P, K * C], U32, align_bytes=64)
         nc.sync.dma_start(
             out=gcn2_words[:].bitcast(I32), in_=gcn2_w_words[0].rearrange("p n t -> p (n t)").bitcast(I32)
@@ -70,7 +71,6 @@ def tile_block_pb_t_kernel(
         for r in range(4):
             nc.sync.dma_start(out=w_scales[r:P:32, C:].bitcast(I32), in_=gcn2_w_scales[0, r:16:4, :].bitcast(I32))
         nc.sync.dma_start(out=gcn2_b_rows[: K * QUARTERS, :], in_=gcn2_b.rearrange("(r n) -> r n", n=P))
-        load_streams(1)
         proj_words = const.tile([P, C], U32, align_bytes=64)
         nc.sync.dma_start(
             out=proj_words[:].bitcast(I32), in_=proj_w_words[0].rearrange("p n t -> p (n t)").bitcast(I32)
@@ -112,16 +112,34 @@ def tile_block_pb_t_kernel(
             )
             nc.vector.quantize_mx(out=adj_codes[:].bitcast(FP8X4), scales=adj_scales[:], in_=adj_grouped[:])
 
-        a_t, g_t, a_scaled, g_plain, g_half, vu, vu_codes, vu_scales = {}, {}, {}, {}, {}, {}, {}, {}
+        g_half, v_in, u_in, v_t, u_t, vu, vu_codes, vu_scales = {}, {}, {}, {}, {}, {}, {}, {}
         y_t_banks, y_t, y_banks, y_grouped, y_codes, y_scales = {}, {}, {}, {}, {}, {}
         out_banks, x_biased, result = {}, {}, {}
 
-        def pairs_by_token(bank):
-            halves = bank[:].rearrange("m s n -> m (s n)").bitcast(BF16)
-            return halves.rearrange("m (s n i) -> m n s i", s=2, i=2)
+        def halve_g(b):
+            g_half[b] = work.tile([P, PAR, C], BF16, name="g_half")
+            nc.vector.tensor_scalar_mul(g_half[b][:], g_in[b][:], S_G2A)
 
-        def by_token(ap):
-            return ap.rearrange("m (n s i) -> m n s i", s=2, i=2)
+        def by_head(ap):
+            return ap.rearrange("p e (h d) -> p e h d", h=H)
+
+        def combine_v(b):
+            v_in[b] = work.tile([P, PAR, C], BF16, name="v_in")
+            nc.vector.tensor_tensor(
+                out=by_head(v_in[b][:]), in0=a_in[b][:].rearrange("p h e d -> p e h d"), in1=by_head(g_half[b][:]), op=ADD
+            )
+
+        def combine_u(b):
+            u_in[b] = work.tile([P, PAR, C], BF16, name="u_in")
+            for e in range(PAR):
+                nc.vector.scalar_tensor_tensor(
+                    out=u_in[b][:, e, :].rearrange("p (h d) -> p h d", h=H),
+                    in0=a_in[b][:, :, e, :],
+                    scalar=S_A2G,
+                    in1=g_in[b][:, e, :].rearrange("p (h d) -> p h d", h=H),
+                    op0=MULT,
+                    op1=ADD,
+                )
 
         def transpose_stream(source, bank):
             words = source[:].rearrange("p e c -> p (e c)").bitcast(F32)
@@ -132,38 +150,25 @@ def tile_block_pb_t_kernel(
                         bank[:, s, e * P : (e + 1) * P], words[:, first : (e + 1) * (C // 2) : 2], identity[:]
                     )
 
-        def transpose_a(b):
-            a_t[b] = psum.tile([P, 2, J], F32, name="a_t")
-            transpose_stream(a_in[b], a_t[b])
+        def transpose_u(b):
+            u_t[b] = psum.tile([P, 2, J], F32, name="u_t")
+            transpose_stream(u_in[b], u_t[b])
 
-        def transpose_g(b):
-            g_t[b] = psum.tile([P, 2, J], F32, name="g_t")
-            transpose_stream(g_in[b], g_t[b])
+        def transpose_v(b):
+            v_t[b] = psum.tile([P, 2, J], F32, name="v_t")
+            transpose_stream(v_in[b], v_t[b])
 
-        def scale_a(b):
-            a_scaled[b] = work.tile([P, 4 * J], F32, name="a_scaled")
-            nc.scalar.activation(out=by_token(a_scaled[b][:]), in_=pairs_by_token(a_t[b]), func=COPY, scale=S_A2G)
-
-        def copy_g(b):
-            g_plain[b] = work.tile([P, 4 * J], BF16, name="g_plain")
+        def group(b, o, bank):
             nc.scalar.copy(
-                out=g_plain[b][:].bitcast(F32).rearrange("m (n s) -> m n s", s=2), in_=g_t[b][:].rearrange("m s n -> m n s")
+                out=vu[b][:, o, :].bitcast(F32).rearrange("m (n s) -> m n s", s=2), in_=bank[:].rearrange("m s n -> m n s")
             )
 
-        def halve_g(b):
-            g_half[b] = work.tile([P, 4 * J], BF16, name="g_half")
-            nc.vector.tensor_scalar_mul(g_half[b][:], g_plain[b][:], S_G2A)
+        def group_u(b):
+            vu[b] = work.tile([P, 2, PACK * J], BF16, name="vu", align_bytes=64)
+            group(b, 1, u_t[b])
 
-        def combine_u(b):
-            vu[b] = work.tile([P, 2, 4 * J], BF16, name="vu", align_bytes=64)
-            nc.vector.tensor_tensor(
-                out=by_token(vu[b][:, 1, :]), in0=pairs_by_token(g_t[b]), in1=by_token(a_scaled[b][:]), op=ADD
-            )
-
-        def combine_v(b):
-            nc.vector.tensor_tensor(
-                out=by_token(vu[b][:, 0, :]), in0=pairs_by_token(a_t[b]), in1=by_token(g_half[b][:]), op=ADD
-            )
+        def group_v(b):
+            group(b, 0, v_t[b])
 
         def quantise_vu(b):
             vu_codes[b] = results.tile([P, 2 * J], U32, name="vu_codes", align_bytes=64)
@@ -266,34 +271,31 @@ def tile_block_pb_t_kernel(
                 load_x(b)
 
         for r in range(-2, B + 1):
-            when(multiply_y, r, 0)
-            when(multiply_y, r, 1)
-            when(bias_y, r, 0)
-            when(bias_y, r, 1)
-            when(combine_u, r + 1)
+            when(combine_u, r + 2)
+            when(bias_x, r)
+            when(transpose_u, r + 1)
+            when(group_u, r + 1)
+            for q in range(3):
+                when(multiply_y, r, q)
+                when(bias_y, r, q)
             when(multiply_out, r - 1, 0)
-            when(multiply_y, r, 2)
-            when(bias_y, r, 2)
-            when(finish, r - 1, 0)
-            when(multiply_out, r - 1, 1)
             when(multiply_y, r, 3)
             when(bias_y, r, 3)
-            when(combine_v, r + 1)
-            when(finish, r - 1, 1)
-            when(transpose_g, r + 2)
-            when(copy_g, r + 2)
-            when(transpose_y, r, 0)
-            when(transpose_y, r, 1)
-            when(group_y, r, 0)
-            when(group_y, r, 1)
-            when(transpose_a, r + 2)
-            when(scale_a, r + 2)
-            when(load_next, r + 2 + AHEAD)
-            when(quantise_vu, r + 1)
+            when(finish, r - 1, 0)
+            when(transpose_v, r + 1)
+            when(group_v, r + 1)
             if r == -1:
                 make_y_bias()
+            when(transpose_y, r, 0)
+            when(group_y, r, 0)
+            when(transpose_y, r, 1)
+            when(group_y, r, 1)
+            when(multiply_out, r - 1, 1)
+            when(quantise_vu, r + 1)
             if r == 0:
                 quantise_adj()
+            when(finish, r - 1, 1)
             when(halve_g, r + 2)
-            when(bias_x, r)
             when(quantise_y, r)
+            when(combine_v, r + 2)
+            when(load_next, r + 2 + AHEAD)

@@ -21,6 +21,7 @@ PAR = J // P
 QUARTERS = C // P
 PACK = 4
 AHEAD = 4
+Y_T_BANKS = 3
 
 FLOPS = 2 * B * J * C * C + 2 * B * J * C * K * C + 2 * B * J * K * J * C
 
@@ -61,6 +62,11 @@ def tile_block_pb_t_kernel(
         nc.vector.memset(gcn2_b_rows[:], 0.0)
         identity = const.tile([P, P], F32)
         make_identity(nc, identity[:])
+        identity_bf16 = const.tile([P, P], BF16)
+        nc.vector.tensor_copy(out=identity_bf16[:], in_=identity[:])
+        first_row_ones = const.tile([P, P], BF16)
+        nc.vector.memset(first_row_ones[:], 0.0)
+        nc.vector.memset(first_row_ones[:1, :], 1.0)
 
         load_streams(0)
         load_streams(1)
@@ -114,7 +120,7 @@ def tile_block_pb_t_kernel(
 
         g_half, v_in, u_in, v_t, u_t, vu, vu_codes, vu_scales = {}, {}, {}, {}, {}, {}, {}, {}
         y_t_banks, y_t, y_banks, y_grouped, y_codes, y_scales = {}, {}, {}, {}, {}, {}
-        out_banks, x_biased, result = {}, {}, {}
+        out_banks, x_banks, x_biased, result = {}, {}, {}, {}
 
         def halve_g(b):
             g_half[b] = work.tile([P, PAR, C], BF16, name="g_half")
@@ -151,11 +157,11 @@ def tile_block_pb_t_kernel(
                     )
 
         def transpose_u(b):
-            u_t[b] = psum.tile([P, 2, J], F32, name="u_t")
+            u_t[b] = psum.tile([P, 2, J], F32, name="stream_t")
             transpose_stream(u_in[b], u_t[b])
 
         def transpose_v(b):
-            v_t[b] = psum.tile([P, 2, J], F32, name="v_t")
+            v_t[b] = psum.tile([P, 2, J], F32, name="stream_t")
             transpose_stream(v_in[b], v_t[b])
 
         def group(b, o, bank):
@@ -177,14 +183,37 @@ def tile_block_pb_t_kernel(
                 out=vu_codes[b][:].bitcast(FP8X4), scales=vu_scales[b][:], in_=vu[b][:].rearrange("m o n -> m (o n)")
             )
 
+        def on_tensor_engine(b):
+            return b % 2 == 0
+
         def bias_x(b):
             x_biased[b] = results.tile([P, PAR, C], F32, name="x_biased")
+            parities = 1 if on_tensor_engine(b) else PAR
             nc.vector.tensor_tensor(
-                out=x_biased[b][:], in0=x_in[b][:], in1=proj_b_rows[:].unsqueeze(1).to_broadcast([P, PAR, C]), op=ADD
+                out=x_biased[b][:, :parities, :],
+                in0=x_in[b][:, :parities, :],
+                in1=proj_b_rows[:].unsqueeze(1).to_broadcast([P, parities, C]),
+                op=ADD,
             )
 
+        y_t_turns = []
+
+        def next_y_t_bank(shape):
+            y_t_turns.append(1)
+            return psum.tile(shape, F32, name="y_t_bank%d" % (len(y_t_turns) % Y_T_BANKS))
+
+        def multiply_x(b):
+            if on_tensor_engine(b):
+                x_banks[b] = next_y_t_bank([P, C])
+                nc.tensor.matmul(x_banks[b][:], lhsT=identity_bf16[:], rhs=x_in[b][:, 1, :], start=True, stop=False)
+                nc.tensor.matmul(x_banks[b][:], lhsT=first_row_ones[:], rhs=proj_b_rows[:], start=False, stop=True)
+
+        def copy_x(b):
+            if on_tensor_engine(b):
+                nc.scalar.copy(out=x_biased[b][:, 1, :], in_=x_banks[b][:])
+
         def multiply_y(b, q):
-            bank = psum.tile([P, K, J], F32, name="y_t_bank%d" % (q % 2))
+            bank = next_y_t_bank([P, K, J])
             y_t_banks[b, q] = bank
             for k in range(K):
                 first = k * C + q * P
@@ -265,37 +294,40 @@ def tile_block_pb_t_kernel(
             if 0 <= b < B:
                 stage(b, *rest)
 
-        def load_next(b):
+        def load_next_streams(b):
             if AHEAD <= b:
                 load_streams(b)
+
+        def load_next_x(b):
+            if AHEAD <= b:
                 load_x(b)
 
-        for r in range(-2, B + 1):
-            when(combine_u, r + 2)
-            when(bias_x, r)
-            when(transpose_u, r + 1)
-            when(group_u, r + 1)
-            for q in range(3):
+        for r in range(-3, B + 1):
+            for q in range(QUARTERS):
                 when(multiply_y, r, q)
                 when(bias_y, r, q)
-            when(multiply_out, r - 1, 0)
-            when(multiply_y, r, 3)
-            when(bias_y, r, 3)
-            when(finish, r - 1, 0)
             when(transpose_v, r + 1)
             when(group_v, r + 1)
+            when(multiply_out, r - 1, 0)
             if r == -1:
                 make_y_bias()
-            when(transpose_y, r, 0)
-            when(group_y, r, 0)
-            when(transpose_y, r, 1)
-            when(group_y, r, 1)
+            for half in range(2):
+                when(transpose_y, r, half)
+                when(group_y, r, half)
+            when(multiply_x, r)
+            when(copy_x, r)
+            when(transpose_u, r + 2)
+            when(group_u, r + 2)
             when(multiply_out, r - 1, 1)
             when(quantise_vu, r + 1)
+            when(finish, r - 1, 0)
+            when(combine_v, r + 2)
+            when(load_next_streams, r + 2 + AHEAD)
             if r == 0:
                 quantise_adj()
-            when(finish, r - 1, 1)
-            when(halve_g, r + 2)
             when(quantise_y, r)
-            when(combine_v, r + 2)
-            when(load_next, r + 2 + AHEAD)
+            when(finish, r - 1, 1)
+            when(halve_g, r + 3)
+            when(combine_u, r + 3)
+            when(bias_x, r + 1)
+            when(load_next_x, r + AHEAD)

@@ -34,20 +34,20 @@ def tile_block_pb_t_kernel(
         const = ctx.enter_context(tc.tile_pool(name="const", bufs=1))
         inputs = ctx.enter_context(tc.tile_pool(name="inputs", bufs=AHEAD))
         work = ctx.enter_context(tc.tile_pool(name="work", bufs=2))
-        results = ctx.enter_context(tc.tile_pool(name="results", bufs=3))
+        results = ctx.enter_context(tc.tile_pool(name="results", bufs=4))
         psum = ctx.enter_context(tc.psum_pool(name="psum", bufs=1))
         ctx.enter_context(tc.manual_schedule())
 
         a_in, g_in, x_in = {}, {}, {}
 
         def load_streams(b):
-            a_in[b] = inputs.tile([P, H, PAR, DH], BF16, name="a_in")
-            nc.sync.dma_start(
-                out=a_in[b][:].rearrange("p h e d -> p h (e d)"), in_=attn_o[b].rearrange("h (p e) d -> p h (e d)", e=PAR)
-            )
             g_in[b] = inputs.tile([P, PAR, C], BF16, name="g_in")
             nc.sync.dma_start(
                 out=g_in[b][:].rearrange("p e c -> p (e c)"), in_=xg1[b].rearrange("(p e) c -> p (e c)", e=PAR)
+            )
+            a_in[b] = inputs.tile([P, H, PAR, DH], BF16, name="a_in")
+            nc.sync.dma_start(
+                out=a_in[b][:].rearrange("p h e d -> p h (e d)"), in_=attn_o[b].rearrange("h (p e) d -> p h (e d)", e=PAR)
             )
 
         def load_x(b):
@@ -77,12 +77,10 @@ def tile_block_pb_t_kernel(
         for r in range(4):
             nc.sync.dma_start(out=w_scales[r:P:32, C:].bitcast(I32), in_=gcn2_w_scales[0, r:16:4, :].bitcast(I32))
         nc.sync.dma_start(out=gcn2_b_rows[: K * QUARTERS, :], in_=gcn2_b.rearrange("(r n) -> r n", n=P))
-        proj_words = const.tile([P, C], U32, align_bytes=64)
-        nc.sync.dma_start(
-            out=proj_words[:].bitcast(I32), in_=proj_w_words[0].rearrange("p n t -> p (n t)").bitcast(I32)
-        )
-        for r in range(4):
-            nc.sync.dma_start(out=w_scales[r:P:32, :C].bitcast(I32), in_=proj_w_scales[0, r:16:4, :].bitcast(I32))
+        load_streams(2)
+        load_x(0)
+        proj_b_rows = const.tile([P, C], BF16)
+        nc.sync.dma_start(out=proj_b_rows[:], in_=proj_b.partition_broadcast(P))
         adj_raw = const.tile([P, PACK, J], BF16)
         for e in range(PAR):
             for k in range(K):
@@ -90,12 +88,14 @@ def tile_block_pb_t_kernel(
                     out=adj_raw[e * P // 2 : (e + 1) * P // 2, 2 * k : 2 * k + 2, :],
                     in_=adj[k].rearrange("(m i e) w -> e m i w", i=2, e=PAR)[e],
                 )
-        proj_b_rows = const.tile([P, C], BF16)
-        nc.sync.dma_start(out=proj_b_rows[:], in_=proj_b.partition_broadcast(P))
-        load_x(0)
-        load_x(1)
-        for b in range(2, AHEAD):
-            load_streams(b)
+        proj_words = const.tile([P, C], U32, align_bytes=64)
+        nc.sync.dma_start(
+            out=proj_words[:].bitcast(I32), in_=proj_w_words[0].rearrange("p n t -> p (n t)").bitcast(I32)
+        )
+        for r in range(4):
+            nc.sync.dma_start(out=w_scales[r:P:32, :C].bitcast(I32), in_=proj_w_scales[0, r:16:4, :].bitcast(I32))
+        load_streams(3)
+        for b in range(1, AHEAD):
             load_x(b)
 
         y_bias = const.tile([P, K * QUARTERS], F32)
@@ -103,7 +103,7 @@ def tile_block_pb_t_kernel(
         def make_y_bias():
             rows = const.tile([P, P], F32)
             nc.vector.tensor_copy(out=rows[:], in_=gcn2_b_rows[:])
-            columns = psum.tile([P, P], F32, name="y_bank0")
+            columns = psum.tile([P, P], F32, name="y_bank1")
             nc.tensor.transpose(columns[:], rows[:], identity[:])
             nc.scalar.copy(out=y_bias[:], in_=columns[:, : K * QUARTERS])
 
@@ -157,7 +157,7 @@ def tile_block_pb_t_kernel(
                     )
 
         def transpose_u(b):
-            u_t[b] = psum.tile([P, 2, J], F32, name="stream_t")
+            u_t[b] = psum.tile([P, 2, J], F32, name="y_bank0" if b == 0 else "stream_t")
             transpose_stream(u_in[b], u_t[b])
 
         def transpose_v(b):
@@ -165,12 +165,13 @@ def tile_block_pb_t_kernel(
             transpose_stream(v_in[b], v_t[b])
 
         def group(b, o, bank):
+            if b not in vu:
+                vu[b] = work.tile([P, 2, PACK * J], BF16, name="vu", align_bytes=64)
             nc.scalar.copy(
                 out=vu[b][:, o, :].bitcast(F32).rearrange("m (n s) -> m n s", s=2), in_=bank[:].rearrange("m s n -> m n s")
             )
 
         def group_u(b):
-            vu[b] = work.tile([P, 2, PACK * J], BF16, name="vu", align_bytes=64)
             group(b, 1, u_t[b])
 
         def group_v(b):
@@ -186,11 +187,15 @@ def tile_block_pb_t_kernel(
         def on_tensor_engine(b):
             return b % 2 == 0
 
+        def biased_tile(b):
+            if b not in x_biased:
+                x_biased[b] = results.tile([P, PAR, C], F32, name="x_biased")
+            return x_biased[b]
+
         def bias_x(b):
-            x_biased[b] = results.tile([P, PAR, C], F32, name="x_biased")
             parities = 1 if on_tensor_engine(b) else PAR
             nc.vector.tensor_tensor(
-                out=x_biased[b][:, :parities, :],
+                out=biased_tile(b)[:, :parities, :],
                 in0=x_in[b][:, :parities, :],
                 in1=proj_b_rows[:].unsqueeze(1).to_broadcast([P, parities, C]),
                 op=ADD,
@@ -210,7 +215,7 @@ def tile_block_pb_t_kernel(
 
         def copy_x(b):
             if on_tensor_engine(b):
-                nc.scalar.copy(out=x_biased[b][:, 1, :], in_=x_banks[b][:])
+                nc.scalar.copy(out=biased_tile(b)[:, 1, :], in_=x_banks[b][:])
 
         def multiply_y(b, q):
             bank = next_y_t_bank([P, K, J])
@@ -290,8 +295,11 @@ def tile_block_pb_t_kernel(
             )
             nc.sync.dma_start(out=out[b].rearrange("(p e) c -> e p c", e=PAR)[f], in_=result[b][:, f, :])
 
+        done = set()
+
         def when(stage, b, *rest):
-            if 0 <= b < B:
+            if 0 <= b < B and (stage, b, rest) not in done:
+                done.add((stage, b, rest))
                 stage(b, *rest)
 
         def load_next_streams(b):
@@ -302,23 +310,48 @@ def tile_block_pb_t_kernel(
             if AHEAD <= b:
                 load_x(b)
 
-        for r in range(-3, B + 1):
-            for q in range(QUARTERS):
+        when(halve_g, 0)
+        when(combine_v, 0)
+        when(combine_u, 0)
+        when(transpose_v, 0)
+        when(group_v, 0)
+        when(transpose_u, 0)
+        when(group_u, 0)
+        when(halve_g, 1)
+        when(combine_u, 1)
+        make_y_bias()
+        when(quantise_vu, 0)
+        when(combine_v, 1)
+        when(transpose_u, 1)
+        when(group_u, 1)
+        for q in range(3):
+            when(multiply_y, 0, q)
+        for q in range(2):
+            when(bias_y, 0, q)
+        when(multiply_y, 0, 3)
+        load_streams(AHEAD)
+
+        for r in range(-1, B + 2):
+            for q in range(2):
+                when(multiply_y, r, q)
+                when(bias_y, r, q)
+            when(multiply_out, r - 2, 1)
+            for q in range(2, QUARTERS):
                 when(multiply_y, r, q)
                 when(bias_y, r, q)
             when(transpose_v, r + 1)
             when(group_v, r + 1)
+            when(transpose_y, r, 0)
+            when(group_y, r, 0)
             when(multiply_out, r - 1, 0)
-            if r == -1:
-                make_y_bias()
-            for half in range(2):
-                when(transpose_y, r, half)
-                when(group_y, r, half)
+            when(transpose_y, r, 1)
+            when(group_y, r, 1)
             when(multiply_x, r)
             when(copy_x, r)
             when(transpose_u, r + 2)
             when(group_u, r + 2)
-            when(multiply_out, r - 1, 1)
+            when(finish, r - 2, 1)
+            when(halve_g, r + 2)
             when(quantise_vu, r + 1)
             when(finish, r - 1, 0)
             when(combine_v, r + 2)
@@ -326,8 +359,6 @@ def tile_block_pb_t_kernel(
             if r == 0:
                 quantise_adj()
             when(quantise_y, r)
-            when(finish, r - 1, 1)
-            when(halve_g, r + 3)
-            when(combine_u, r + 3)
-            when(bias_x, r + 1)
+            when(bias_x, r)
             when(load_next_x, r + AHEAD)
+            when(combine_u, r + 3)

@@ -185,7 +185,7 @@ def tile_block_pb_t_kernel(
             )
 
         def on_tensor_engine(b):
-            return b % 2 == 0
+            return b % 2 == 0 or b == B - 1
 
         def biased_tile(b):
             if b not in x_biased:
@@ -239,7 +239,7 @@ def tile_block_pb_t_kernel(
                 laid_out = y_t[b][:, q, k, :]
                 joints = y_t_banks[b, q][:, k, :]
                 column = y_bias[:, k * QUARTERS + q : k * QUARTERS + q + 1]
-                if b == B - 1 and q % 2 == 1:
+                if b == B - 1 and q == 3:
                     nc.vector.tensor_scalar(out=laid_out, in0=joints, scalar1=column, scalar2=None, op0=ADD)
                 else:
                     nc.scalar.activation(out=laid_out, in_=joints, func=IDENTITY, bias=column)
@@ -312,18 +312,18 @@ def tile_block_pb_t_kernel(
 
         when(halve_g, 0)
         when(combine_v, 0)
-        when(combine_u, 0)
         when(transpose_v, 0)
         when(group_v, 0)
+        when(combine_u, 0)
         when(transpose_u, 0)
         when(group_u, 0)
-        when(halve_g, 1)
         when(combine_u, 1)
-        make_y_bias()
-        when(quantise_vu, 0)
-        when(combine_v, 1)
         when(transpose_u, 1)
         when(group_u, 1)
+        make_y_bias()
+        when(halve_g, 1)
+        when(quantise_vu, 0)
+        when(combine_v, 1)
         for q in range(3):
             when(multiply_y, 0, q)
         for q in range(2):
@@ -331,7 +331,7 @@ def tile_block_pb_t_kernel(
         when(multiply_y, 0, 3)
         load_streams(AHEAD)
 
-        for r in range(-1, B + 2):
+        for r in range(-1, B - 1):
             for q in range(2):
                 when(multiply_y, r, q)
                 when(bias_y, r, q)
@@ -362,3 +362,31 @@ def tile_block_pb_t_kernel(
             when(bias_x, r)
             when(load_next_x, r + AHEAD)
             when(combine_u, r + 3)
+
+        last = B - 1
+        multiply_y(last, 0)
+        multiply_out(last - 2, 1)
+        multiply_y(last, 1)
+        bias_y(last, 0)
+        multiply_y(last, 2)
+        multiply_y(last, 3)
+        bias_y(last, 1)
+        multiply_out(last - 1, 0)
+        bias_y(last, 2)
+        finish(last - 2, 1)
+        transpose_y(last, 0)
+        group_y(last, 0)
+        bias_y(last, 3)
+        transpose_y(last, 1)
+        finish(last - 1, 0)
+        multiply_x(last)
+        bias_x(last)
+        group_y(last, 1)
+        copy_x(last)
+        quantise_y(last)
+        multiply_out(last - 1, 1)
+        multiply_out(last, 0)
+        finish(last - 1, 1)
+        finish(last, 0)
+        multiply_out(last, 1)
+        finish(last, 1)

@@ -69,14 +69,14 @@ def tile_block_pb_t_kernel(
         nc.vector.memset(first_row_ones[:1, :], 1.0)
 
         load_streams(0)
+        for r in range(4):
+            nc.sync.dma_start(out=w_scales[r:P:32, C:].bitcast(I32), in_=gcn2_w_scales[0, r:16:4, :].bitcast(I32))
+        nc.sync.dma_start(out=gcn2_b_rows[: K * QUARTERS, :], in_=gcn2_b.rearrange("(r n) -> r n", n=P))
         load_streams(1)
         gcn2_words = const.tile([P, K * C], U32, align_bytes=64)
         nc.sync.dma_start(
             out=gcn2_words[:].bitcast(I32), in_=gcn2_w_words[0].rearrange("p n t -> p (n t)").bitcast(I32)
         )
-        for r in range(4):
-            nc.sync.dma_start(out=w_scales[r:P:32, C:].bitcast(I32), in_=gcn2_w_scales[0, r:16:4, :].bitcast(I32))
-        nc.sync.dma_start(out=gcn2_b_rows[: K * QUARTERS, :], in_=gcn2_b.rearrange("(r n) -> r n", n=P))
         load_streams(2)
         load_x(0)
         proj_b_rows = const.tile([P, C], BF16)

@@ -185,7 +185,7 @@ def tile_block_pb_t_kernel(
             )
 
         def on_tensor_engine(b):
-            return b % 2 == 0 or b == B - 1
+            return b % 3 != 1
 
         def biased_tile(b):
             if b not in x_biased:

from contextlib import ExitStack

import concourse.mybir as mybir
from concourse.masks import make_identity

F32 = mybir.dt.float32
BF16 = mybir.dt.bfloat16
I32 = mybir.dt.int32
U32 = mybir.dt.uint32
U8 = mybir.dt.uint8
FP8X4 = mybir.dt.float8_e4m3fn_x4
ADD = mybir.AluOpType.add
MULT = mybir.AluOpType.mult
IDENTITY = mybir.ActivationFunctionType.Identity

P = 128
B, J, C, K, H = 16, 256, 512, 2, 8
DH = C // H
S_G2A, S_A2G = 0.5, 0.8
PAR = J // P
QUARTERS = C // P
PACK = 4
AHEAD = 4
Y_T_BANKS = 3

FLOPS = 2 * B * J * C * C + 2 * B * J * C * K * C + 2 * B * J * K * J * C


def tile_block_pb_t_kernel(
    tc, attn_o, xg1, x, adj, proj_w_words, proj_w_scales, proj_b, gcn2_w_words, gcn2_w_scales, gcn2_b, out
):
    nc = tc.nc
    with ExitStack() as ctx:
        const = ctx.enter_context(tc.tile_pool(name="const", bufs=1))
        inputs = ctx.enter_context(tc.tile_pool(name="inputs", bufs=AHEAD))
        work = ctx.enter_context(tc.tile_pool(name="work", bufs=2))
        results = ctx.enter_context(tc.tile_pool(name="results", bufs=4))
        psum = ctx.enter_context(tc.psum_pool(name="psum", bufs=1))
        ctx.enter_context(tc.manual_schedule())

        a_in, g_in, x_in = {}, {}, {}

        def load_streams(b):
            g_in[b] = inputs.tile([P, PAR, C], BF16, name="g_in")
            nc.sync.dma_start(
                out=g_in[b][:].rearrange("p e c -> p (e c)"), in_=xg1[b].rearrange("(p e) c -> p (e c)", e=PAR)
            )
            a_in[b] = inputs.tile([P, H, PAR, DH], BF16, name="a_in")
            nc.sync.dma_start(
                out=a_in[b][:].rearrange("p h e d -> p h (e d)"), in_=attn_o[b].rearrange("h (p e) d -> p h (e d)", e=PAR)
            )

        def load_x(b):
            x_in[b] = inputs.tile([P, PAR, C], BF16, name="x_in")
            nc.sync.dma_start(
                out=x_in[b][:].rearrange("p e c -> p (e c)"), in_=x[b].rearrange("(p e) c -> p (e c)", e=PAR)
            )

        w_scales = const.tile([P, C + K * C], U8, align_bytes=64)
        nc.vector.memset(w_scales[:].bitcast(I32), 0)
        gcn2_b_rows = const.tile([P, P], BF16)
        nc.vector.memset(gcn2_b_rows[:], 0.0)
        identity = const.tile([P, P], F32)
        make_identity(nc, identity[:])
        identity_bf16 = const.tile([P, P], BF16)
        nc.vector.tensor_copy(out=identity_bf16[:], in_=identity[:])
        first_row_ones = const.tile([P, P], BF16)
        nc.vector.memset(first_row_ones[:], 0.0)
        nc.vector.memset(first_row_ones[:1, :], 1.0)

        load_streams(0)
        for r in range(4):
            nc.sync.dma_start(out=w_scales[r:P:32, C:].bitcast(I32), in_=gcn2_w_scales[0, r:16:4, :].bitcast(I32))
        nc.sync.dma_start(out=gcn2_b_rows[: K * QUARTERS, :], in_=gcn2_b.rearrange("(r n) -> r n", n=P))
        load_streams(1)
        gcn2_words = const.tile([P, K * C], U32, align_bytes=64)
        nc.sync.dma_start(
            out=gcn2_words[:].bitcast(I32), in_=gcn2_w_words[0].rearrange("p n t -> p (n t)").bitcast(I32)
        )
        load_streams(2)
        load_x(0)
        proj_b_rows = const.tile([P, C], BF16)
        nc.sync.dma_start(out=proj_b_rows[:], in_=proj_b.partition_broadcast(P))
        adj_raw = const.tile([P, PACK, J], BF16)
        for e in range(PAR):
            for k in range(K):
                nc.sync.dma_start(
                    out=adj_raw[e * P // 2 : (e + 1) * P // 2, 2 * k : 2 * k + 2, :],
                    in_=adj[k].rearrange("(m i e) w -> e m i w", i=2, e=PAR)[e],
                )
        proj_words = const.tile([P, C], U32, align_bytes=64)
        nc.sync.dma_start(
            out=proj_words[:].bitcast(I32), in_=proj_w_words[0].rearrange("p n t -> p (n t)").bitcast(I32)
        )
        for r in range(4):
            nc.sync.dma_start(out=w_scales[r:P:32, :C].bitcast(I32), in_=proj_w_scales[0, r:16:4, :].bitcast(I32))
        load_streams(3)
        for b in range(1, AHEAD):
            load_x(b)

        y_bias = const.tile([P, K * QUARTERS], F32)

        def make_y_bias():
            rows = const.tile([P, P], F32)
            nc.vector.tensor_copy(out=rows[:], in_=gcn2_b_rows[:])
            columns = psum.tile([P, P], F32, name="y_bank1")
            nc.tensor.transpose(columns[:], rows[:], identity[:])
            nc.scalar.copy(out=y_bias[:], in_=columns[:, : K * QUARTERS])

        adj_codes = const.tile([P, J], U32, align_bytes=64)
        adj_scales = const.tile([P, J], U8, align_bytes=64)

        def quantise_adj():
            adj_grouped = const.tile([P, J * PACK], BF16, align_bytes=64)
            nc.vector.tensor_copy(
                out=adj_grouped[:].rearrange("p (f m t) -> p f m t", f=PAR, t=PACK),
                in_=adj_raw[:].rearrange("p t (m f) -> p f m t", f=PAR),
            )
            nc.vector.quantize_mx(out=adj_codes[:].bitcast(FP8X4), scales=adj_scales[:], in_=adj_grouped[:])

        g_half, v_in, u_in, v_t, u_t, vu, vu_codes, vu_scales = {}, {}, {}, {}, {}, {}, {}, {}
        y_t_banks, y_t, y_banks, y_grouped, y_codes, y_scales = {}, {}, {}, {}, {}, {}
        out_banks, x_banks, x_biased, result = {}, {}, {}, {}

        def halve_g(b):
            g_half[b] = work.tile([P, PAR, C], BF16, name="g_half")
            nc.vector.tensor_scalar_mul(g_half[b][:], g_in[b][:], S_G2A)

        def by_head(ap):
            return ap.rearrange("p e (h d) -> p e h d", h=H)

        def combine_v(b):
            v_in[b] = work.tile([P, PAR, C], BF16, name="v_in")
            nc.vector.tensor_tensor(
                out=by_head(v_in[b][:]), in0=a_in[b][:].rearrange("p h e d -> p e h d"), in1=by_head(g_half[b][:]), op=ADD
            )

        def combine_u(b):
            u_in[b] = work.tile([P, PAR, C], BF16, name="u_in")
            for e in range(PAR):
                nc.vector.scalar_tensor_tensor(
                    out=u_in[b][:, e, :].rearrange("p (h d) -> p h d", h=H),
                    in0=a_in[b][:, :, e, :],
                    scalar=S_A2G,
                    in1=g_in[b][:, e, :].rearrange("p (h d) -> p h d", h=H),
                    op0=MULT,
                    op1=ADD,
                )

        def transpose_stream(source, bank):
            words = source[:].rearrange("p e c -> p (e c)").bitcast(F32)
            for e in range(PAR):
                for s in range(2):
                    first = e * (C // 2) + s
                    nc.tensor.transpose(
                        bank[:, s, e * P : (e + 1) * P], words[:, first : (e + 1) * (C // 2) : 2], identity[:]
                    )

        def transpose_u(b):
            u_t[b] = psum.tile([P, 2, J], F32, name="y_bank0" if b == 0 else "stream_t")
            transpose_stream(u_in[b], u_t[b])

        def transpose_v(b):
            v_t[b] = psum.tile([P, 2, J], F32, name="stream_t")
            transpose_stream(v_in[b], v_t[b])

        def group(b, o, bank):
            if b not in vu:
                vu[b] = work.tile([P, 2, PACK * J], BF16, name="vu", align_bytes=64)
            nc.scalar.copy(
                out=vu[b][:, o, :].bitcast(F32).rearrange("m (n s) -> m n s", s=2), in_=bank[:].rearrange("m s n -> m n s")
            )

        def group_u(b):
            group(b, 1, u_t[b])

        def group_v(b):
            group(b, 0, v_t[b])

        def quantise_vu(b):
            vu_codes[b] = results.tile([P, 2 * J], U32, name="vu_codes", align_bytes=64)
            vu_scales[b] = results.tile([P, 2 * J], U8, name="vu_scales", align_bytes=64)
            nc.vector.quantize_mx(
                out=vu_codes[b][:].bitcast(FP8X4), scales=vu_scales[b][:], in_=vu[b][:].rearrange("m o n -> m (o n)")
            )

        def on_tensor_engine(b):
            return b % 3 != 1

        def biased_tile(b):
            if b not in x_biased:
                x_biased[b] = results.tile([P, PAR, C], F32, name="x_biased")
            return x_biased[b]

        def bias_x(b):
            parities = 1 if on_tensor_engine(b) else PAR
            nc.vector.tensor_tensor(
                out=biased_tile(b)[:, :parities, :],
                in0=x_in[b][:, :parities, :],
                in1=proj_b_rows[:].unsqueeze(1).to_broadcast([P, parities, C]),
                op=ADD,
            )

        y_t_turns = []

        def next_y_t_bank(shape):
            y_t_turns.append(1)
            return psum.tile(shape, F32, name="y_t_bank%d" % (len(y_t_turns) % Y_T_BANKS))

        def multiply_x(b):
            if on_tensor_engine(b):
                x_banks[b] = next_y_t_bank([P, C])
                nc.tensor.matmul(x_banks[b][:], lhsT=identity_bf16[:], rhs=x_in[b][:, 1, :], start=True, stop=False)
                nc.tensor.matmul(x_banks[b][:], lhsT=first_row_ones[:], rhs=proj_b_rows[:], start=False, stop=True)

        def copy_x(b):
            if on_tensor_engine(b):
                nc.scalar.copy(out=biased_tile(b)[:, 1, :], in_=x_banks[b][:])

        def multiply_y(b, q):
            bank = next_y_t_bank([P, K, J])
            y_t_banks[b, q] = bank
            for k in range(K):
                first = k * C + q * P
                nc.tensor.matmul_mx(
                    out=bank[:, k, :],
                    lhsT=gcn2_words[:, first : first + P].bitcast(FP8X4),
                    lhsT_scale=w_scales[:, C + first : C + first + P],
                    rhs=vu_codes[b][:, J:].bitcast(FP8X4),
                    rhs_scale=vu_scales[b][:, J:],
                    start=True,
                    stop=True,
                )

        def bias_y(b, q):
            if q == 0:
                y_t[b] = work.tile([P, QUARTERS, K, J], BF16, name="y_t")
            for k in range(K):
                laid_out = y_t[b][:, q, k, :]
                joints = y_t_banks[b, q][:, k, :]
                column = y_bias[:, k * QUARTERS + q : k * QUARTERS + q + 1]
                if b == B - 1 and q == 3:
                    nc.vector.tensor_scalar(out=laid_out, in0=joints, scalar1=column, scalar2=None, op0=ADD)
                else:
                    nc.scalar.activation(out=laid_out, in_=joints, func=IDENTITY, bias=column)

        def transpose_y(b, half):
            bank = psum.tile([P, 2, K, P], F32, name="y_bank%d" % half)
            y_banks[b, half] = bank
            for i in range(2):
                for k in range(K):
                    nc.tensor.transpose(bank[:, i, k, :], y_t[b][:, 2 * half + i, k, :].bitcast(F32), identity[:])

        def group_y(b, half):
            if half == 0:
                y_grouped[b] = work.tile([P, PACK * C], BF16, name="y_grouped", align_bytes=64)
            part = slice(half * PACK * C // 2, (half + 1) * PACK * C // 2)
            words = y_grouped[b][:, part].bitcast(F32).rearrange("p (i c k) -> p i c k", i=2, k=K)
            source = y_banks[b, half][:].rearrange("p i k c -> p i c k")
            nc.scalar.copy(out=words, in_=source)

        def quantise_y(b):
            y_codes[b] = work.tile([P, C], U32, name="y_codes", align_bytes=64)
            y_scales[b] = work.tile([P, C], U8, name="y_scales", align_bytes=64)
            nc.vector.quantize_mx(out=y_codes[b][:].bitcast(FP8X4), scales=y_scales[b][:], in_=y_grouped[b][:])

        def multiply_out(b, f):
            bank = psum.tile([P, C], F32, name="out_bank%d" % f)
            out_banks[b, f] = bank
            tokens = slice(f * P, (f + 1) * P)
            nc.tensor.matmul_mx(
                out=bank[:],
                lhsT=vu_codes[b][:, tokens].bitcast(FP8X4),
                lhsT_scale=vu_scales[b][:, tokens],
                rhs=proj_words[:].bitcast(FP8X4),
                rhs_scale=w_scales[:, :C],
                start=True,
                stop=False,
            )
            nc.tensor.matmul_mx(
                out=bank[:],
                lhsT=adj_codes[:, tokens].bitcast(FP8X4),
                lhsT_scale=adj_scales[:, tokens],
                rhs=y_codes[b][:].bitcast(FP8X4),
                rhs_scale=y_scales[b][:],
                start=False,
                stop=True,
            )

        def finish(b, f):
            if f == 0:
                result[b] = results.tile([P, PAR, C], F32, name="result")
            nc.vector.tensor_tensor(
                out=result[b][:, f, :], in0=out_banks[b, f][:], in1=x_biased[b][:, f, :], op=ADD
            )
            nc.sync.dma_start(out=out[b].rearrange("(p e) c -> e p c", e=PAR)[f], in_=result[b][:, f, :])

        done = set()

        def when(stage, b, *rest):
            if 0 <= b < B and (stage, b, rest) not in done:
                done.add((stage, b, rest))
                stage(b, *rest)

        def load_next_streams(b):
            if AHEAD <= b:
                load_streams(b)

        def load_next_x(b):
            if AHEAD <= b:
                load_x(b)

        when(halve_g, 0)
        when(combine_v, 0)
        when(transpose_v, 0)
        when(group_v, 0)
        when(combine_u, 0)
        when(transpose_u, 0)
        when(group_u, 0)
        when(combine_u, 1)
        when(transpose_u, 1)
        when(group_u, 1)
        make_y_bias()
        when(halve_g, 1)
        when(quantise_vu, 0)
        when(combine_v, 1)
        for q in range(3):
            when(multiply_y, 0, q)
        for q in range(2):
            when(bias_y, 0, q)
        when(multiply_y, 0, 3)
        load_streams(AHEAD)

        for r in range(-1, B - 1):
            for q in range(2):
                when(multiply_y, r, q)
                when(bias_y, r, q)
            when(multiply_out, r - 2, 1)
            for q in range(2, QUARTERS):
                when(multiply_y, r, q)
                when(bias_y, r, q)
            when(transpose_v, r + 1)
            when(group_v, r + 1)
            when(transpose_y, r, 0)
            when(group_y, r, 0)
            when(multiply_out, r - 1, 0)
            when(transpose_y, r, 1)
            when(group_y, r, 1)
            when(multiply_x, r)
            when(copy_x, r)
            when(transpose_u, r + 2)
            when(group_u, r + 2)
            when(finish, r - 2, 1)
            when(halve_g, r + 2)
            when(quantise_vu, r + 1)
            when(finish, r - 1, 0)
            when(combine_v, r + 2)
            when(load_next_streams, r + 2 + AHEAD)
            if r == 0:
                quantise_adj()
            when(quantise_y, r)
            when(bias_x, r)
            when(load_next_x, r + AHEAD)
            when(combine_u, r + 3)

        last = B - 1
        multiply_y(last, 0)
        multiply_out(last - 2, 1)
        multiply_y(last, 1)
        bias_y(last, 0)
        multiply_y(last, 2)
        multiply_y(last, 3)
        bias_y(last, 1)
        multiply_out(last - 1, 0)
        bias_y(last, 2)
        finish(last - 2, 1)
        transpose_y(last, 0)
        group_y(last, 0)
        bias_y(last, 3)
        transpose_y(last, 1)
        finish(last - 1, 0)
        multiply_x(last)
        bias_x(last)
        group_y(last, 1)
        copy_x(last)
        quantise_y(last)
        multiply_out(last - 1, 1)
        multiply_out(last, 0)
        finish(last - 1, 1)
        finish(last, 0)
        multiply_out(last, 1)
        finish(last, 1)
